import numpy as np
import ml_dtypes


def mxq(x, axis, fmt="e4m3"):
    dtype, down = {"e4m3": (ml_dtypes.float8_e4m3fn, 7), "e5m2": (ml_dtypes.float8_e5m2, 14)}[fmt]
    v = np.moveaxis(np.asarray(x, np.float32).astype(ml_dtypes.bfloat16).astype(np.float64), axis, -1)
    blocks = v.reshape(v.shape[:-1] + (-1, 32))
    amax = np.abs(blocks).max(-1, keepdims=True)
    byte = np.maximum(np.where(amax > 0, np.frexp(amax)[1] - 1 + 127, 0) - down, 1)
    scale = np.exp2(byte - 127.0)
    codes = (blocks / scale).astype(np.float32).astype(dtype).astype(np.float64)
    return np.moveaxis((codes * scale).reshape(v.shape), -1, axis)


WIDE = False


def mx_kscale(k):
    if not WIDE:
        return np.ones(k)
    levels = np.array([10, -10, 5, -5, 0])
    a = np.random.permutation(np.resize(levels, k // 512 * 4)).reshape(k // 512, 4)
    idx = np.arange(k)
    return np.exp2(a[idx // 512, idx % 128 // 32])


BF16 = ml_dtypes.bfloat16


def bf(x):
    return np.asarray(x, np.float32).astype(BF16)


def f64(x):
    return np.asarray(x).astype(np.float64)


B, S, D_MODEL, N_HEADS, D_KV, D_ROPE = 2, 128, 5120, 8, 512, 16
D_HEAD = D_MODEL // N_HEADS
SPLIT = D_HEAD - D_ROPE
ROT_SCALE = 40.0
ROT_BASE = 10000.0


def rotate_half(x):
    x1, x2 = np.split(x, 2, axis=-1)
    return np.concatenate((-x2, x1), axis=-1)


def apply_rotary(x, cos, sin):
    r = cos.shape[-1]
    x_rot, x_base = x[..., :r], x[..., r:]
    x_rot = x_rot * cos + rotate_half(x_rot) * sin
    return np.concatenate((x_rot, x_base), axis=-1)


def rotary_emb(seq_len):
    exps = np.arange(0, D_ROPE // 2, 2, dtype=np.float64) / (D_ROPE // 2)
    inv_freq = 1.0 / ROT_BASE ** exps
    t = np.arange(seq_len, dtype=np.float64) / ROT_SCALE
    freqs = t[:, None] * inv_freq[None, :]
    return np.concatenate((freqs, freqs), axis=-1)


def setup_inputs():
    s = mx_kscale(D_MODEL)
    return {
        "h": bf(np.random.standard_normal((B, S, D_MODEL)) * s),
        "W_dkv": bf(np.random.standard_normal((D_MODEL, D_KV)) / np.sqrt(D_MODEL) / s[:, None]),
        "b_dkv": bf(np.random.standard_normal(D_KV) * 0.3),
        "W_uk": bf(np.random.standard_normal((D_KV, N_HEADS * SPLIT)) / np.sqrt(D_KV)),
        "b_uk": bf(np.random.standard_normal(N_HEADS * SPLIT) * 0.3),
        "W_uv": bf(np.random.standard_normal((D_KV, N_HEADS * D_HEAD)) / np.sqrt(D_KV)),
        "b_uv": bf(np.random.standard_normal(N_HEADS * D_HEAD) * 0.3),
        "W_kr": bf(np.random.standard_normal((D_MODEL, N_HEADS * D_ROPE)) * 2.0 / np.sqrt(D_MODEL) / s[:, None]),
        "b_kr": bf(np.random.standard_normal(N_HEADS * D_ROPE) * 0.5),
    }


def reference(h, W_dkv, b_dkv, W_uk, b_uk, W_uv, b_uv, W_kr, b_kr):
    hq = mxq(f64(h), 2, "e4m3")
    c_kv = (hq @ mxq(f64(W_dkv), 0, "e4m3")) + f64(b_dkv)
    cq = mxq(c_kv, 2, "e4m3")
    k = ((cq @ mxq(f64(W_uk), 0, "e4m3")) + f64(b_uk)).reshape(B, S, N_HEADS, SPLIT)
    v = ((cq @ mxq(f64(W_uv), 0, "e4m3")) + f64(b_uv)).reshape(B, S, N_HEADS, D_HEAD)
    k_rot = ((hq @ mxq(f64(W_kr), 0, "e4m3")) + f64(b_kr)).reshape(B, S, N_HEADS, D_ROPE)
    emb = rotary_emb(S)
    cos = np.cos(emb).reshape(1, S, 1, -1)
    sin = np.sin(emb).reshape(1, S, 1, -1)
    k_rot = apply_rotary(k_rot, cos, sin)
    k_full = np.concatenate((k, k_rot), axis=-1)
    return k_full, v, c_kv, k_rot

@@ -1,0 +1,353 @@
+from contextlib import ExitStack
+
+import concourse.mybir as mybir
+from concourse.masks import make_identity
+
+F32 = mybir.dt.float32
+BF16 = mybir.dt.bfloat16
+I32 = mybir.dt.int32
+U32 = mybir.dt.uint32
+U8 = mybir.dt.uint8
+FP8X4 = mybir.dt.float8_e4m3fn_x4
+ADD = mybir.AluOpType.add
+MULT = mybir.AluOpType.mult
+SIN = mybir.ActivationFunctionType.Sin
+
+P = 128
+PACK = 4
+K_PASS = P * PACK
+BATCH = 2
+D_MODEL = 5120
+D_KV = 512
+HEADS = 8
+D_HEAD = 640
+D_ROPE = 16
+D_NOPE = D_HEAD - D_ROPE
+ROT = D_ROPE // 2
+ROT_SCALE = 40.0
+
+PASSES = D_MODEL // K_PASS
+GROUP = 2
+GROUPS = PASSES // GROUP
+GROUP_K = GROUP * K_PASS
+
+CHUNK_HEADS = 2
+CHUNK = CHUNK_HEADS * D_HEAD
+CHUNKS = HEADS // CHUNK_HEADS
+QUANT_WORDS = (1024, 256)
+PASS_COLS = (512, 512, 256)
+VECTOR_COLS = 96
+
+BIAS_ROWS = 2 * HEADS + 1
+FIRST_ROW = 2 * HEADS
+
+FLOPS = 2 * BATCH * P * (D_MODEL * (D_KV + HEADS * D_ROPE) + D_KV * HEADS * (D_NOPE + D_HEAD))
+
+
+def regroup(copy, grouped, rows):
+    copy(
+        out=grouped.rearrange("p (c i) t -> p c t i", i=4),
+        in_=rows.rearrange("p t (c i) -> p c t i", i=4),
+    )
+
+
+def quantise(nc, grouped, codes, scales, words):
+    start = 0
+    for count in words:
+        nc.vector.quantize_mx(
+            out=codes[:, start : start + count].bitcast(FP8X4),
+            scales=scales[:, start : start + count],
+            in_=grouped[:, PACK * start : PACK * (start + count)],
+        )
+        start += count
+
+
+def tile_mla_pb_kernel(
+    tc, h, W_dkv, b_dkv, W_uk, b_uk, W_uv, b_uv, W_kr, b_kr, out_0, out_1, out_2, out_3
+):
+    nc = tc.nc
+    with ExitStack() as ctx:
+        keep = ctx.enter_context(tc.tile_pool(name="keep", bufs=1))
+        h_in = ctx.enter_context(tc.tile_pool(name="h_in", bufs=3))
+        wd_in = ctx.enter_context(tc.tile_pool(name="wd_in", bufs=3))
+        wu_in = ctx.enter_context(tc.tile_pool(name="wu_in", bufs=4))
+        h_stage = ctx.enter_context(tc.tile_pool(name="h_stage", bufs=2))
+        w_stage = ctx.enter_context(tc.tile_pool(name="w_stage", bufs=3))
+        w_quant = ctx.enter_context(tc.tile_pool(name="w_quant", bufs=3))
+        outs = ctx.enter_context(tc.tile_pool(name="outs", bufs=6))
+        psum = ctx.enter_context(tc.psum_pool(name="psum", bufs=8))
+
+        ident_f32 = keep.tile([P, P], F32, name="ident_f32")
+        make_identity(nc, ident_f32[:])
+        ident_bf = keep.tile([P, P], BF16, name="ident_bf")
+        make_identity(nc, ident_bf[:])
+
+        bias_rows = keep.tile([P, D_HEAD], BF16, name="bias_rows")
+        nc.vector.memset(bias_rows[:], 0.0)
+        nc.scalar.dma_start(
+            out=bias_rows[FIRST_ROW : FIRST_ROW + 1, 0:D_KV],
+            in_=b_dkv.rearrange("(o n) -> o n", o=1),
+        )
+        nc.scalar.dma_start(
+            out=bias_rows[FIRST_ROW : FIRST_ROW + 1, D_KV:D_HEAD],
+            in_=b_kr.rearrange("(o n) -> o n", o=1),
+        )
+        nc.scalar.dma_start(
+            out=bias_rows[0:HEADS, 0:D_NOPE], in_=b_uk.rearrange("(r n) -> r n", r=HEADS)
+        )
+        nc.scalar.dma_start(
+            out=bias_rows[HEADS : 2 * HEADS, :], in_=b_uv.rearrange("(r n) -> r n", r=HEADS)
+        )
+        bias_all = keep.tile([P, BIAS_ROWS * D_HEAD], BF16, name="bias_all")
+
+        def spread_bias_row(r):
+            pick_row = ident_bf[:, r : r + 1].to_broadcast([P, P])
+            spread = psum.tile([P, D_HEAD], BF16, name="spread", tag="bank")
+            nc.tensor.matmul(
+                out=spread[:, 0:512], lhsT=pick_row, rhs=bias_rows[:, 0:512], start=True, stop=True
+            )
+            nc.tensor.matmul(
+                out=spread[:, 512:D_HEAD],
+                lhsT=pick_row,
+                rhs=bias_rows[:, 512:D_HEAD],
+                start=True,
+                stop=True,
+            )
+            nc.scalar.copy(out=bias_all[:, r * D_HEAD : (r + 1) * D_HEAD], in_=spread[:])
+
+        pos_int = keep.tile([P, 1], I32, name="pos_int")
+        nc.gpsimd.iota(pos_int[:], pattern=[[0, 1]], base=0, channel_multiplier=1)
+        pos = keep.tile([P, 1], F32, name="pos")
+        nc.vector.tensor_copy(out=pos[:], in_=pos_int[:])
+        half_angle = keep.tile([P, ROT // 2], F32, name="half_angle")
+        for j in range(ROT // 2):
+            nc.vector.memset(half_angle[:, j : j + 1], 2.0 * ROT_SCALE * 10.0**j)
+        nc.vector.reciprocal(out=half_angle[:], in_=half_angle[:])
+        nc.vector.tensor_scalar(
+            out=half_angle[:], in0=half_angle[:], scalar1=pos[:, 0:1], scalar2=None, op0=MULT
+        )
+        sin_half = keep.tile([P, ROT // 2], F32, name="sin_half")
+        nc.scalar.activation(out=sin_half[:], in_=half_angle[:], func=SIN)
+        sin_quarter = keep.tile([P, ROT // 2], F32, name="sin_quarter")
+        nc.scalar.activation(out=sin_quarter[:], in_=half_angle[:], func=SIN, scale=0.5)
+        cos_half = keep.tile([P, ROT // 2], F32, name="cos_half")
+        nc.vector.tensor_tensor(out=cos_half[:], in0=sin_quarter[:], in1=sin_quarter[:], op=MULT)
+        nc.vector.tensor_scalar(
+            out=cos_half[:], in0=cos_half[:], scalar1=-2.0, scalar2=1.0, op0=MULT, op1=ADD
+        )
+        half_sin = keep.tile([P, ROT // 2], F32, name="half_sin")
+        nc.vector.tensor_tensor(out=half_sin[:], in0=sin_half[:], in1=cos_half[:], op=MULT)
+        sin_sq = keep.tile([P, ROT // 2], F32, name="sin_sq")
+        nc.vector.tensor_tensor(out=sin_sq[:], in0=sin_half[:], in1=sin_half[:], op=MULT)
+        rot_cos = keep.tile([P, ROT], F32, name="rot_cos")
+        rot_sin = keep.tile([P, ROT], F32, name="rot_sin")
+        for half, sign in ((0, -2.0), (1, 2.0)):
+            cols = slice(half * ROT // 2, (half + 1) * ROT // 2)
+            nc.vector.tensor_scalar(
+                out=rot_cos[:, cols], in0=sin_sq[:], scalar1=-2.0, scalar2=1.0, op0=MULT, op1=ADD
+            )
+            nc.vector.tensor_scalar(
+                out=rot_sin[:, cols], in0=half_sin[:], scalar1=sign, scalar2=None, op0=MULT
+            )
+
+        spread_bias_row(FIRST_ROW)
+
+        h_codes = keep.tile([P, PASSES * BATCH * P], U32, name="h_codes", align_bytes=64)
+        h_scales = keep.tile([P, PASSES * BATCH * P], U8, name="h_scales", align_bytes=64)
+        h_tokens = h.rearrange("a r k -> r a k")
+        c_acc = [psum.tile([P, D_KV], F32, name="c_acc%d" % a, tag="bank") for a in range(BATCH)]
+
+        for g in range(GROUPS):
+            h_raw = h_in.tile([P, BATCH * GROUP_K], BF16, name="h_raw")
+            nc.sync.dma_start(
+                out=h_raw[:].rearrange("r (a k) -> r a k", a=BATCH),
+                in_=h_tokens[:, :, g * GROUP_K : (g + 1) * GROUP_K],
+            )
+            wd_raw = wd_in.tile([P, GROUP, PACK, D_KV], BF16, name="wd_raw")
+            nc.sync.dma_start(
+                out=wd_raw[:],
+                in_=W_dkv[g * GROUP_K : (g + 1) * GROUP_K, :].rearrange(
+                    "(c p t) n -> p c t n", c=GROUP, p=P, t=PACK
+                ),
+            )
+
+            h_words = h_raw[:].bitcast(F32).rearrange("r (a m) -> r a m", a=BATCH)
+            h_grouped = h_stage.tile([P, GROUP * BATCH * P * PACK], BF16, name="h_grouped", align_bytes=64)
+            h_grouped_words = h_grouped[:].bitcast(F32).rearrange(
+                "p (c a r u) -> p c a r u", c=GROUP, a=BATCH, r=P
+            )
+            for c in range(GROUP):
+                hT = psum.tile([P, BATCH, 2, P], F32, name="hT", tag="bank")
+                first_word = c * K_PASS // 2
+                for a in range(BATCH):
+                    for u in range(2):
+                        nc.tensor.transpose(
+                            hT[:, a, u, :],
+                            h_words[:, a, first_word + u : first_word + K_PASS // 2 : 2],
+                            ident_f32[:],
+                        )
+                nc.scalar.copy(out=h_grouped_words[:, c], in_=hT[:].rearrange("p a u r -> p a r u"))
+            group_words = slice(g * GROUP * BATCH * P, (g + 1) * GROUP * BATCH * P)
+            nc.vector.quantize_mx(
+                out=h_codes[:, group_words].bitcast(FP8X4),
+                scales=h_scales[:, group_words],
+                in_=h_grouped[:],
+            )
+
+            wd_grouped = w_stage.tile([P, GROUP * D_KV * PACK], BF16, name="wd_grouped", tag="grouped", align_bytes=64)
+            wd_view = wd_grouped[:].rearrange("p (c n t) -> p c n t", c=GROUP, t=PACK)
+            regroup(nc.vector.tensor_copy, wd_view[:, 0], wd_raw[:, 0])
+            regroup(nc.scalar.copy, wd_view[:, 1], wd_raw[:, 1])
+            wd_codes = w_quant.tile([P, GROUP * D_KV], U32, name="wd_codes", tag="codes", align_bytes=64)
+            wd_scales = w_quant.tile([P, GROUP * D_KV], U8, name="wd_scales", tag="scales", align_bytes=64)
+            quantise(nc, wd_grouped, wd_codes, wd_scales, (GROUP * D_KV,))
+
+            for c in range(GROUP):
+                s = g * GROUP + c
+                for a in range(BATCH):
+                    tokens = slice((s * BATCH + a) * P, (s * BATCH + a + 1) * P)
+                    nc.tensor.matmul_mx(
+                        out=c_acc[a][:],
+                        lhsT=h_codes[:, tokens].bitcast(FP8X4),
+                        lhsT_scale=h_scales[:, tokens],
+                        rhs=wd_codes[:, c * D_KV : (c + 1) * D_KV].bitcast(FP8X4),
+                        rhs_scale=wd_scales[:, c * D_KV : (c + 1) * D_KV],
+                        start=(s == 0),
+                        stop=(s == PASSES - 1),
+                    )
+
+        KR = HEADS * D_ROPE
+        wr_raw = wu_in.tile([P, PASSES, PACK, KR], BF16, name="wr_raw", tag="wu_raw")
+        nc.sync.dma_start(
+            out=wr_raw[:], in_=W_kr.rearrange("(s p t) n -> p s t n", s=PASSES, p=P, t=PACK)
+        )
+        wr_grouped = w_stage.tile([P, PASSES * KR * PACK], BF16, name="wr_grouped", tag="grouped", align_bytes=64)
+        nc.vector.tensor_copy(
+            out=wr_grouped[:].rearrange("p (s c i t) -> p s c t i", s=PASSES, i=4, t=PACK),
+            in_=wr_raw[:].rearrange("p s t (c i) -> p s c t i", i=4),
+        )
+        wr_codes = keep.tile([P, PASSES * KR], U32, name="wr_codes", align_bytes=64)
+        wr_scales = keep.tile([P, PASSES * KR], U8, name="wr_scales", align_bytes=64)
+        quantise(nc, wr_grouped, wr_codes, wr_scales, QUANT_WORDS)
+
+        first_bias = bias_all[:, FIRST_ROW * D_HEAD : (FIRST_ROW + 1) * D_HEAD]
+        c_f32 = keep.tile([P, BATCH, D_KV], F32, name="c_f32")
+        c_bf = keep.tile([P, BATCH, PACK, P], BF16, name="c_bf")
+        c_grouped = keep.tile([P, BATCH * P * PACK], BF16, name="c_grouped", align_bytes=64)
+        c_grouped_view = c_grouped[:].rearrange("q (a r t) -> q a r t", a=BATCH, t=PACK)
+        for a in range(BATCH):
+            nc.vector.tensor_tensor(out=c_f32[:, a, :], in0=c_acc[a][:], in1=first_bias[:, 0:D_KV], op=ADD)
+            nc.sync.dma_start(out=out_2[a], in_=c_f32[:, a, :])
+            nc.scalar.copy(out=c_bf[:, a], in_=c_f32[:, a, :].rearrange("r (q t) -> r t q", t=PACK))
+            cT = psum.tile([P, PACK, P], BF16, name="cT", tag="bank")
+            for t in range(PACK):
+                nc.tensor.transpose(cT[:, t, :], c_bf[:, a, t, :], ident_bf[:])
+            nc.vector.tensor_copy(out=c_grouped_view[:, a], in_=cT[:].rearrange("q t r -> q r t"))
+        c_codes = keep.tile([P, BATCH * P], U32, name="c_codes", align_bytes=64)
+        c_scales = keep.tile([P, BATCH * P], U8, name="c_scales", align_bytes=64)
+        quantise(nc, c_grouped, c_codes, c_scales, (BATCH * P,))
+
+        kr_acc = psum.tile([P, BATCH, KR], F32, name="kr_acc", tag="bank")
+        for a in range(BATCH):
+            for s in range(PASSES):
+                tokens = slice((s * BATCH + a) * P, (s * BATCH + a + 1) * P)
+                nc.tensor.matmul_mx(
+                    out=kr_acc[:, a, :],
+                    lhsT=h_codes[:, tokens].bitcast(FP8X4),
+                    lhsT_scale=h_scales[:, tokens],
+                    rhs=wr_codes[:, s * KR : (s + 1) * KR].bitcast(FP8X4),
+                    rhs_scale=wr_scales[:, s * KR : (s + 1) * KR],
+                    start=(s == 0),
+                    stop=(s == PASSES - 1),
+                )
+        k_rot = keep.tile([P, BATCH, HEADS, D_ROPE], F32, name="k_rot")
+        nc.vector.tensor_tensor(
+            out=k_rot[:].rearrange("r a e d -> r a (e d)"),
+            in0=kr_acc[:],
+            in1=first_bias[:, D_KV:D_HEAD].unsqueeze(1).to_broadcast([P, BATCH, KR]),
+            op=ADD,
+        )
+        x = k_rot[:].rearrange("r a e d -> r (a e) d")
+        rows = BATCH * HEADS
+        kept = keep.tile([P, rows, ROT], F32, name="kept")
+        turned = keep.tile([P, rows, ROT], F32, name="turned")
+        nc.vector.tensor_tensor(
+            out=kept[:], in0=x[:, :, 0:ROT], in1=rot_cos[:].unsqueeze(1).to_broadcast([P, rows, ROT]), op=MULT
+        )
+        nc.vector.tensor_tensor(
+            out=turned[:, :, 0 : ROT // 2],
+            in0=x[:, :, ROT // 2 : ROT],
+            in1=rot_sin[:, 0 : ROT // 2].unsqueeze(1).to_broadcast([P, rows, ROT // 2]),
+            op=MULT,
+        )
+        nc.vector.tensor_tensor(
+            out=turned[:, :, ROT // 2 : ROT],
+            in0=x[:, :, 0 : ROT // 2],
+            in1=rot_sin[:, ROT // 2 : ROT].unsqueeze(1).to_broadcast([P, rows, ROT // 2]),
+            op=MULT,
+        )
+        nc.vector.tensor_tensor(out=x[:, :, 0:ROT], in0=kept[:], in1=turned[:], op=ADD)
+        nc.sync.dma_start(
+            out=out_3.rearrange("a r e d -> r a (e d)"), in_=k_rot[:].rearrange("r a e d -> r a (e d)")
+        )
+
+        for r in range(2 * HEADS):
+            spread_bias_row(r)
+
+        for which, (weight, head_cols, out) in enumerate(((W_uk, D_NOPE, out_0), (W_uv, D_HEAD, out_1))):
+            weight_rows = weight.rearrange("(p t) n -> p t n", t=PACK)
+            for i in range(CHUNKS):
+                wu_raw = wu_in.tile([P, PACK, CHUNK_HEADS * head_cols], BF16, name="wu_raw", tag="wu_raw")
+                nc.sync.dma_start(
+                    out=wu_raw[:],
+                    in_=weight_rows[:, :, i * CHUNK_HEADS * head_cols : (i + 1) * CHUNK_HEADS * head_cols],
+                )
+                wu_grouped = w_stage.tile([P, CHUNK * PACK], BF16, name="wu_grouped", tag="grouped", align_bytes=64)
+                wu_view = wu_grouped[:].rearrange("p (e n t) -> p e n t", e=CHUNK_HEADS, t=PACK)
+                split = head_cols - VECTOR_COLS
+                for e in range(CHUNK_HEADS):
+                    first = e * head_cols
+                    regroup(nc.scalar.copy, wu_view[:, e, 0:split, :], wu_raw[:, :, first : first + split])
+                    regroup(
+                        nc.vector.tensor_copy,
+                        wu_view[:, e, split:head_cols, :],
+                        wu_raw[:, :, first + split : first + head_cols],
+                    )
+                    if head_cols < D_HEAD:
+                        nc.vector.memset(wu_view[:, e, head_cols:D_HEAD, :], 0.0)
+                wu_codes = w_quant.tile([P, CHUNK], U32, name="wu_codes", tag="codes", align_bytes=64)
+                wu_scales = w_quant.tile([P, CHUNK], U8, name="wu_scales", tag="scales", align_bytes=64)
+                quantise(nc, wu_grouped, wu_codes, wu_scales, QUANT_WORDS)
+
+                first_bias_col = (which * HEADS + i * CHUNK_HEADS) * D_HEAD
+                for a in range(BATCH):
+                    result = outs.tile([P, CHUNK_HEADS, D_HEAD], F32, name="result")
+                    result_flat = result[:].rearrange("r e d -> r (e d)")
+                    start = 0
+                    for count in PASS_COLS:
+                        acc = psum.tile([P, count], F32, name="acc", tag="bank")
+                        nc.tensor.matmul_mx(
+                            out=acc[:],
+                            lhsT=c_codes[:, a * P : (a + 1) * P].bitcast(FP8X4),
+                            lhsT_scale=c_scales[:, a * P : (a + 1) * P],
+                            rhs=wu_codes[:, start : start + count].bitcast(FP8X4),
+                            rhs_scale=wu_scales[:, start : start + count],
+                            start=True,
+                            stop=True,
+                        )
+                        nc.vector.tensor_tensor(
+                            out=result_flat[:, start : start + count],
+                            in0=acc[:],
+                            in1=bias_all[:, first_bias_col + start : first_bias_col + start + count],
+                            op=ADD,
+                        )
+                        start += count
+                    if head_cols < D_HEAD:
+                        nc.vector.tensor_copy(
+                            out=result[:, :, head_cols:D_HEAD],
+                            in_=k_rot[:, a, i * CHUNK_HEADS : (i + 1) * CHUNK_HEADS, :],
+                        )
+                    nc.sync.dma_start(
+                        out=out[a, :, i * CHUNK_HEADS : (i + 1) * CHUNK_HEADS, :].rearrange("r e d -> r (e d)"),
+                        in_=result_flat,
+                    )

@@ -36,8 +36,12 @@ CHUNK = CHUNK_HEADS * D_HEAD
 CHUNKS = HEADS // CHUNK_HEADS
 QUANT_WORDS = (1024, 256)
 PASS_COLS = (512, 512, 256)
-VECTOR_COLS = 96
+VECTOR_COLS = 128
+WD_SCALAR_COLS = 160
 
+H_BUFS = 3
+WU_BUFS = 4
+OUT_BUFS = 6
 BIAS_ROWS = 2 * HEADS + 1
 FIRST_ROW = 2 * HEADS
 
@@ -68,55 +72,100 @@ def tile_mla_pb_kernel(
     nc = tc.nc
     with ExitStack() as ctx:
         keep = ctx.enter_context(tc.tile_pool(name="keep", bufs=1))
-        h_in = ctx.enter_context(tc.tile_pool(name="h_in", bufs=3))
-        wd_in = ctx.enter_context(tc.tile_pool(name="wd_in", bufs=3))
-        wu_in = ctx.enter_context(tc.tile_pool(name="wu_in", bufs=4))
+        h_in = ctx.enter_context(tc.tile_pool(name="h_in", bufs=H_BUFS))
+        wd_in = ctx.enter_context(tc.tile_pool(name="wd_in", bufs=H_BUFS))
+        wu_in = ctx.enter_context(tc.tile_pool(name="wu_in", bufs=WU_BUFS))
         h_stage = ctx.enter_context(tc.tile_pool(name="h_stage", bufs=2))
         w_stage = ctx.enter_context(tc.tile_pool(name="w_stage", bufs=3))
         w_quant = ctx.enter_context(tc.tile_pool(name="w_quant", bufs=3))
-        outs = ctx.enter_context(tc.tile_pool(name="outs", bufs=6))
+        outs = ctx.enter_context(tc.tile_pool(name="outs", bufs=OUT_BUFS))
         psum = ctx.enter_context(tc.psum_pool(name="psum", bufs=8))
+        ctx.enter_context(tc.manual_schedule())
 
+        h_tokens = h.rearrange("a r k -> r a k")
+        h_raw = {}
+        wd_raw = {}
+        wu_raw = {}
+
+        def load_h(g):
+            h_raw[g] = h_in.tile([P, BATCH * GROUP_K], BF16, name="h_raw")
+            nc.sync.dma_start(
+                out=h_raw[g][:].rearrange("r (a k) -> r a k", a=BATCH),
+                in_=h_tokens[:, :, g * GROUP_K : (g + 1) * GROUP_K],
+            )
+
+        def load_wd(g):
+            wd_raw[g] = wd_in.tile([P, GROUP, PACK, D_KV], BF16, name="wd_raw")
+            nc.sync.dma_start(
+                out=wd_raw[g][:],
+                in_=W_dkv[g * GROUP_K : (g + 1) * GROUP_K, :].rearrange(
+                    "(c p t) n -> p c t n", c=GROUP, p=P, t=PACK
+                ),
+            )
+
+        def chunk_source(n):
+            if n < CHUNKS:
+                return W_uv, D_HEAD, out_1, HEADS + n * CHUNK_HEADS, n
+            return W_uk, D_NOPE, out_0, (n - CHUNKS) * CHUNK_HEADS, n - CHUNKS
+
+        def load_chunk(n):
+            weight, head_cols, out, bias_row, i = chunk_source(n)
+            wu_raw[n] = wu_in.tile([P, PACK, CHUNK_HEADS * head_cols], BF16, name="wu_raw")
+            nc.sync.dma_start(
+                out=wu_raw[n][:],
+                in_=weight.rearrange("(p t) n -> p t n", t=PACK)[
+                    :, :, i * CHUNK_HEADS * head_cols : (i + 1) * CHUNK_HEADS * head_cols
+                ],
+            )
+
+        load_wd(0)
+        load_h(0)
+        bias_rows = keep.tile([P, D_HEAD], BF16, name="bias_rows")
+        nc.vector.memset(bias_rows[:], 0.0)
+        nc.sync.dma_start(
+            out=bias_rows[FIRST_ROW : FIRST_ROW + 1, 0:D_KV],
+            in_=b_dkv.rearrange("(o n) -> o n", o=1),
+        )
+        nc.sync.dma_start(
+            out=bias_rows[FIRST_ROW : FIRST_ROW + 1, D_KV:D_HEAD],
+            in_=b_kr.rearrange("(o n) -> o n", o=1),
+        )
+        nc.sync.dma_start(
+            out=bias_rows[HEADS : 2 * HEADS, :], in_=b_uv.rearrange("(r n) -> r n", r=HEADS)
+        )
+        nc.sync.dma_start(
+            out=bias_rows[0:HEADS, 0:D_NOPE], in_=b_uk.rearrange("(r n) -> r n", r=HEADS)
+        )
+        for g in range(1, H_BUFS):
+            load_wd(g)
+            load_h(g)
+
+        pos_int = keep.tile([P, 1], I32, name="pos_int")
+        nc.gpsimd.iota(pos_int[:], pattern=[[0, 1]], base=0, channel_multiplier=1)
         ident_f32 = keep.tile([P, P], F32, name="ident_f32")
         make_identity(nc, ident_f32[:])
         ident_bf = keep.tile([P, P], BF16, name="ident_bf")
         make_identity(nc, ident_bf[:])
 
-        bias_rows = keep.tile([P, D_HEAD], BF16, name="bias_rows")
-        nc.vector.memset(bias_rows[:], 0.0)
-        nc.scalar.dma_start(
-            out=bias_rows[FIRST_ROW : FIRST_ROW + 1, 0:D_KV],
-            in_=b_dkv.rearrange("(o n) -> o n", o=1),
-        )
-        nc.scalar.dma_start(
-            out=bias_rows[FIRST_ROW : FIRST_ROW + 1, D_KV:D_HEAD],
-            in_=b_kr.rearrange("(o n) -> o n", o=1),
-        )
-        nc.scalar.dma_start(
-            out=bias_rows[0:HEADS, 0:D_NOPE], in_=b_uk.rearrange("(r n) -> r n", r=HEADS)
-        )
-        nc.scalar.dma_start(
-            out=bias_rows[HEADS : 2 * HEADS, :], in_=b_uv.rearrange("(r n) -> r n", r=HEADS)
-        )
         bias_all = keep.tile([P, BIAS_ROWS * D_HEAD], BF16, name="bias_all")
+        bias_order = [FIRST_ROW] + list(range(HEADS, 2 * HEADS)) + list(range(HEADS))
 
-        def spread_bias_row(r):
-            pick_row = ident_bf[:, r : r + 1].to_broadcast([P, P])
-            spread = psum.tile([P, D_HEAD], BF16, name="spread", tag="bank")
-            nc.tensor.matmul(
-                out=spread[:, 0:512], lhsT=pick_row, rhs=bias_rows[:, 0:512], start=True, stop=True
-            )
-            nc.tensor.matmul(
-                out=spread[:, 512:D_HEAD],
-                lhsT=pick_row,
-                rhs=bias_rows[:, 512:D_HEAD],
-                start=True,
-                stop=True,
-            )
-            nc.scalar.copy(out=bias_all[:, r * D_HEAD : (r + 1) * D_HEAD], in_=spread[:])
+        def spread_two_bias_rows(step):
+            for r in bias_order[2 * step : 2 * step + 2]:
+                pick_row = ident_bf[:, r : r + 1].to_broadcast([P, P])
+                spread = psum.tile([P, D_HEAD], BF16, name="spread", tag="bank")
+                nc.tensor.matmul(
+                    out=spread[:, 0:512], lhsT=pick_row, rhs=bias_rows[:, 0:512], start=True, stop=True
+                )
+                nc.tensor.matmul(
+                    out=spread[:, 512:D_HEAD],
+                    lhsT=pick_row,
+                    rhs=bias_rows[:, 512:D_HEAD],
+                    start=True,
+                    stop=True,
+                )
+                nc.scalar.copy(out=bias_all[:, r * D_HEAD : (r + 1) * D_HEAD], in_=spread[:])
 
-        pos_int = keep.tile([P, 1], I32, name="pos_int")
-        nc.gpsimd.iota(pos_int[:], pattern=[[0, 1]], base=0, channel_multiplier=1)
         pos = keep.tile([P, 1], F32, name="pos")
         nc.vector.tensor_copy(out=pos[:], in_=pos_int[:])
         half_angle = keep.tile([P, ROT // 2], F32, name="half_angle")
@@ -130,50 +179,40 @@ def tile_mla_pb_kernel(
         nc.scalar.activation(out=sin_half[:], in_=half_angle[:], func=SIN)
         sin_quarter = keep.tile([P, ROT // 2], F32, name="sin_quarter")
         nc.scalar.activation(out=sin_quarter[:], in_=half_angle[:], func=SIN, scale=0.5)
+        rot_cos = keep.tile([P, ROT], F32, name="rot_cos")
+        rot_sin = keep.tile([P, ROT], F32, name="rot_sin")
+
         cos_half = keep.tile([P, ROT // 2], F32, name="cos_half")
-        nc.vector.tensor_tensor(out=cos_half[:], in0=sin_quarter[:], in1=sin_quarter[:], op=MULT)
-        nc.vector.tensor_scalar(
+        nc.gpsimd.tensor_tensor(out=cos_half[:], in0=sin_quarter[:], in1=sin_quarter[:], op=MULT)
+        nc.gpsimd.tensor_scalar(
             out=cos_half[:], in0=cos_half[:], scalar1=-2.0, scalar2=1.0, op0=MULT, op1=ADD
         )
         half_sin = keep.tile([P, ROT // 2], F32, name="half_sin")
-        nc.vector.tensor_tensor(out=half_sin[:], in0=sin_half[:], in1=cos_half[:], op=MULT)
+        nc.gpsimd.tensor_tensor(out=half_sin[:], in0=sin_half[:], in1=cos_half[:], op=MULT)
         sin_sq = keep.tile([P, ROT // 2], F32, name="sin_sq")
-        nc.vector.tensor_tensor(out=sin_sq[:], in0=sin_half[:], in1=sin_half[:], op=MULT)
-        rot_cos = keep.tile([P, ROT], F32, name="rot_cos")
-        rot_sin = keep.tile([P, ROT], F32, name="rot_sin")
+        nc.gpsimd.tensor_tensor(out=sin_sq[:], in0=sin_half[:], in1=sin_half[:], op=MULT)
         for half, sign in ((0, -2.0), (1, 2.0)):
             cols = slice(half * ROT // 2, (half + 1) * ROT // 2)
-            nc.vector.tensor_scalar(
+            nc.gpsimd.tensor_scalar(
                 out=rot_cos[:, cols], in0=sin_sq[:], scalar1=-2.0, scalar2=1.0, op0=MULT, op1=ADD
             )
-            nc.vector.tensor_scalar(
+            nc.gpsimd.tensor_scalar(
                 out=rot_sin[:, cols], in0=half_sin[:], scalar1=sign, scalar2=None, op0=MULT
             )
 
-        spread_bias_row(FIRST_ROW)
 
         h_codes = keep.tile([P, PASSES * BATCH * P], U32, name="h_codes", align_bytes=64)
         h_scales = keep.tile([P, PASSES * BATCH * P], U8, name="h_scales", align_bytes=64)
-        h_tokens = h.rearrange("a r k -> r a k")
         c_acc = [psum.tile([P, D_KV], F32, name="c_acc%d" % a, tag="bank") for a in range(BATCH)]
+        h_grouped = {}
+        grouped = {}
+        codes = {}
+        scales = {}
 
-        for g in range(GROUPS):
-            h_raw = h_in.tile([P, BATCH * GROUP_K], BF16, name="h_raw")
-            nc.sync.dma_start(
-                out=h_raw[:].rearrange("r (a k) -> r a k", a=BATCH),
-                in_=h_tokens[:, :, g * GROUP_K : (g + 1) * GROUP_K],
-            )
-            wd_raw = wd_in.tile([P, GROUP, PACK, D_KV], BF16, name="wd_raw")
-            nc.sync.dma_start(
-                out=wd_raw[:],
-                in_=W_dkv[g * GROUP_K : (g + 1) * GROUP_K, :].rearrange(
-                    "(c p t) n -> p c t n", c=GROUP, p=P, t=PACK
-                ),
-            )
-
-            h_words = h_raw[:].bitcast(F32).rearrange("r (a m) -> r a m", a=BATCH)
-            h_grouped = h_stage.tile([P, GROUP * BATCH * P * PACK], BF16, name="h_grouped", align_bytes=64)
-            h_grouped_words = h_grouped[:].bitcast(F32).rearrange(
+        def transpose_h(g):
+            h_words = h_raw[g][:].bitcast(F32).rearrange("r (a m) -> r a m", a=BATCH)
+            h_grouped[g] = h_stage.tile([P, GROUP * BATCH * P * PACK], BF16, name="h_grouped", align_bytes=64)
+            h_grouped_words = h_grouped[g][:].bitcast(F32).rearrange(
                 "p (c a r u) -> p c a r u", c=GROUP, a=BATCH, r=P
             )
             for c in range(GROUP):
@@ -187,21 +226,26 @@ def tile_mla_pb_kernel(
                             ident_f32[:],
                         )
                 nc.scalar.copy(out=h_grouped_words[:, c], in_=hT[:].rearrange("p a u r -> p a r u"))
+
+        def regroup_wd(g):
+            grouped[g] = w_stage.tile([P, GROUP * D_KV * PACK], BF16, name="wd_grouped", tag="grouped", align_bytes=64)
+            wd_view = grouped[g][:].rearrange("p (c n t) -> p c n t", c=GROUP, t=PACK)
+            for c in range(GROUP):
+                regroup(nc.scalar.copy, wd_view[:, c, 0:WD_SCALAR_COLS, :], wd_raw[g][:, c, :, 0:WD_SCALAR_COLS])
+                regroup(nc.vector.tensor_copy, wd_view[:, c, WD_SCALAR_COLS:D_KV, :], wd_raw[g][:, c, :, WD_SCALAR_COLS:D_KV])
+
+        def quantise_group(g):
             group_words = slice(g * GROUP * BATCH * P, (g + 1) * GROUP * BATCH * P)
             nc.vector.quantize_mx(
                 out=h_codes[:, group_words].bitcast(FP8X4),
                 scales=h_scales[:, group_words],
-                in_=h_grouped[:],
+                in_=h_grouped[g][:],
             )
+            codes[g] = w_quant.tile([P, GROUP * D_KV], U32, name="wd_codes", tag="codes", align_bytes=64)
+            scales[g] = w_quant.tile([P, GROUP * D_KV], U8, name="wd_scales", tag="scales", align_bytes=64)
+            quantise(nc, grouped[g], codes[g], scales[g], (GROUP * D_KV,))
 
-            wd_grouped = w_stage.tile([P, GROUP * D_KV * PACK], BF16, name="wd_grouped", tag="grouped", align_bytes=64)
-            wd_view = wd_grouped[:].rearrange("p (c n t) -> p c n t", c=GROUP, t=PACK)
-            regroup(nc.vector.tensor_copy, wd_view[:, 0], wd_raw[:, 0])
-            regroup(nc.scalar.copy, wd_view[:, 1], wd_raw[:, 1])
-            wd_codes = w_quant.tile([P, GROUP * D_KV], U32, name="wd_codes", tag="codes", align_bytes=64)
-            wd_scales = w_quant.tile([P, GROUP * D_KV], U8, name="wd_scales", tag="scales", align_bytes=64)
-            quantise(nc, wd_grouped, wd_codes, wd_scales, (GROUP * D_KV,))
-
+        def multiply_c(g):
             for c in range(GROUP):
                 s = g * GROUP + c
                 for a in range(BATCH):
@@ -210,144 +254,186 @@ def tile_mla_pb_kernel(
                         out=c_acc[a][:],
                         lhsT=h_codes[:, tokens].bitcast(FP8X4),
                         lhsT_scale=h_scales[:, tokens],
-                        rhs=wd_codes[:, c * D_KV : (c + 1) * D_KV].bitcast(FP8X4),
-                        rhs_scale=wd_scales[:, c * D_KV : (c + 1) * D_KV],
+                        rhs=codes[g][:, c * D_KV : (c + 1) * D_KV].bitcast(FP8X4),
+                        rhs_scale=scales[g][:, c * D_KV : (c + 1) * D_KV],
                         start=(s == 0),
                         stop=(s == PASSES - 1),
                     )
 
-        KR = HEADS * D_ROPE
-        wr_raw = wu_in.tile([P, PASSES, PACK, KR], BF16, name="wr_raw", tag="wu_raw")
-        nc.sync.dma_start(
-            out=wr_raw[:], in_=W_kr.rearrange("(s p t) n -> p s t n", s=PASSES, p=P, t=PACK)
-        )
-        wr_grouped = w_stage.tile([P, PASSES * KR * PACK], BF16, name="wr_grouped", tag="grouped", align_bytes=64)
-        nc.vector.tensor_copy(
-            out=wr_grouped[:].rearrange("p (s c i t) -> p s c t i", s=PASSES, i=4, t=PACK),
-            in_=wr_raw[:].rearrange("p s t (c i) -> p s c t i", i=4),
-        )
-        wr_codes = keep.tile([P, PASSES * KR], U32, name="wr_codes", align_bytes=64)
-        wr_scales = keep.tile([P, PASSES * KR], U8, name="wr_scales", align_bytes=64)
-        quantise(nc, wr_grouped, wr_codes, wr_scales, QUANT_WORDS)
+        c_codes = keep.tile([P, BATCH * P], U32, name="c_codes", align_bytes=64)
+        c_scales = keep.tile([P, BATCH * P], U8, name="c_scales", align_bytes=64)
+        k_rot = keep.tile([P, BATCH, HEADS, D_ROPE], F32, name="k_rot")
+        wu_grouped = {}
+        wu_codes = {}
+        wu_scales = {}
+
+        def regroup_chunk(n):
+            weight, head_cols, out, bias_row, i = chunk_source(n)
+            wu_grouped[n] = w_stage.tile([P, CHUNK * PACK], BF16, name="wu_grouped", tag="grouped", align_bytes=64)
+            wu_view = wu_grouped[n][:].rearrange("p (e n t) -> p e n t", e=CHUNK_HEADS, t=PACK)
+            split = head_cols - VECTOR_COLS
+            for e in range(CHUNK_HEADS):
+                first = e * head_cols
+                regroup(nc.scalar.copy, wu_view[:, e, 0:split, :], wu_raw[n][:, :, first : first + split])
+                regroup(
+                    nc.vector.tensor_copy,
+                    wu_view[:, e, split:head_cols, :],
+                    wu_raw[n][:, :, first + split : first + head_cols],
+                )
+                if head_cols < D_HEAD:
+                    nc.gpsimd.memset(wu_view[:, e, head_cols:D_HEAD, :], 0.0)
+
+        def quantise_chunk(n):
+            wu_codes[n] = w_quant.tile([P, CHUNK], U32, name="wu_codes", tag="codes", align_bytes=64)
+            wu_scales[n] = w_quant.tile([P, CHUNK], U8, name="wu_scales", tag="scales", align_bytes=64)
+            quantise(nc, wu_grouped[n], wu_codes[n], wu_scales[n], QUANT_WORDS)
+
+        def multiply_chunk(n):
+            weight, head_cols, out, bias_row, i = chunk_source(n)
+            for a in range(BATCH):
+                result = outs.tile([P, CHUNK_HEADS, D_HEAD], F32, name="result")
+                result_flat = result[:].rearrange("r e d -> r (e d)")
+                start = 0
+                for count in PASS_COLS:
+                    acc = psum.tile([P, count], F32, name="acc", tag="bank")
+                    nc.tensor.matmul_mx(
+                        out=acc[:],
+                        lhsT=c_codes[:, a * P : (a + 1) * P].bitcast(FP8X4),
+                        lhsT_scale=c_scales[:, a * P : (a + 1) * P],
+                        rhs=wu_codes[n][:, start : start + count].bitcast(FP8X4),
+                        rhs_scale=wu_scales[n][:, start : start + count],
+                        start=True,
+                        stop=True,
+                    )
+                    nc.vector.tensor_tensor(
+                        out=result_flat[:, start : start + count],
+                        in0=acc[:],
+                        in1=bias_all[:, bias_row * D_HEAD + start : bias_row * D_HEAD + start + count],
+                        op=ADD,
+                    )
+                    start += count
+                if head_cols < D_HEAD:
+                    nc.gpsimd.tensor_copy(
+                        out=result[:, :, head_cols:D_HEAD],
+                        in_=k_rot[:, a, i * CHUNK_HEADS : (i + 1) * CHUNK_HEADS, :],
+                    )
+                nc.sync.dma_start(
+                    out=out[a, :, i * CHUNK_HEADS : (i + 1) * CHUNK_HEADS, :].rearrange("r e d -> r (e d)"),
+                    in_=result_flat,
+                )
 
         first_bias = bias_all[:, FIRST_ROW * D_HEAD : (FIRST_ROW + 1) * D_HEAD]
         c_f32 = keep.tile([P, BATCH, D_KV], F32, name="c_f32")
         c_bf = keep.tile([P, BATCH, PACK, P], BF16, name="c_bf")
         c_grouped = keep.tile([P, BATCH * P * PACK], BF16, name="c_grouped", align_bytes=64)
         c_grouped_view = c_grouped[:].rearrange("q (a r t) -> q a r t", a=BATCH, t=PACK)
-        for a in range(BATCH):
+
+        def finish_c(a):
             nc.vector.tensor_tensor(out=c_f32[:, a, :], in0=c_acc[a][:], in1=first_bias[:, 0:D_KV], op=ADD)
             nc.sync.dma_start(out=out_2[a], in_=c_f32[:, a, :])
+
+        def transpose_c(a):
             nc.scalar.copy(out=c_bf[:, a], in_=c_f32[:, a, :].rearrange("r (q t) -> r t q", t=PACK))
             cT = psum.tile([P, PACK, P], BF16, name="cT", tag="bank")
             for t in range(PACK):
                 nc.tensor.transpose(cT[:, t, :], c_bf[:, a, t, :], ident_bf[:])
-            nc.vector.tensor_copy(out=c_grouped_view[:, a], in_=cT[:].rearrange("q t r -> q r t"))
-        c_codes = keep.tile([P, BATCH * P], U32, name="c_codes", align_bytes=64)
-        c_scales = keep.tile([P, BATCH * P], U8, name="c_scales", align_bytes=64)
-        quantise(nc, c_grouped, c_codes, c_scales, (BATCH * P,))
+            nc.scalar.copy(out=c_grouped_view[:, a], in_=cT[:].rearrange("q t r -> q r t"))
 
-        kr_acc = psum.tile([P, BATCH, KR], F32, name="kr_acc", tag="bank")
+        KR = HEADS * D_ROPE
+        wr_raw = keep.tile([P, PASSES, PACK, KR], BF16, name="wr_raw")
+        wr_codes = keep.tile([P, PASSES * KR], U32, name="wr_codes", align_bytes=64)
+        wr_scales = keep.tile([P, PASSES * KR], U8, name="wr_scales", align_bytes=64)
+
+        def regroup_wr():
+            wr_grouped = w_stage.tile([P, PASSES * KR * PACK], BF16, name="wr_grouped", tag="grouped", align_bytes=64)
+            nc.vector.tensor_copy(
+                out=wr_grouped[:].rearrange("p (s c i t) -> p s c t i", s=PASSES, i=4, t=PACK),
+                in_=wr_raw[:].rearrange("p s t (c i) -> p s c t i", i=4),
+            )
+            return wr_grouped
+
+        def multiply_rope():
+            kr_acc = psum.tile([P, BATCH, KR], F32, name="kr_acc", tag="bank")
+            for a in range(BATCH):
+                for s in range(PASSES):
+                    tokens = slice((s * BATCH + a) * P, (s * BATCH + a + 1) * P)
+                    nc.tensor.matmul_mx(
+                        out=kr_acc[:, a, :],
+                        lhsT=h_codes[:, tokens].bitcast(FP8X4),
+                        lhsT_scale=h_scales[:, tokens],
+                        rhs=wr_codes[:, s * KR : (s + 1) * KR].bitcast(FP8X4),
+                        rhs_scale=wr_scales[:, s * KR : (s + 1) * KR],
+                        start=(s == 0),
+                        stop=(s == PASSES - 1),
+                    )
+            return kr_acc
+
+        def rotate(kr_acc):
+            nc.vector.tensor_tensor(
+                out=k_rot[:].rearrange("r a e d -> r a (e d)"),
+                in0=kr_acc[:],
+                in1=first_bias[:, D_KV:D_HEAD].unsqueeze(1).to_broadcast([P, BATCH, KR]),
+                op=ADD,
+            )
+            x = k_rot[:].rearrange("r a e d -> r (a e) d")
+            rows = BATCH * HEADS
+            kept = keep.tile([P, rows, ROT], F32, name="kept")
+            turned = keep.tile([P, rows, ROT], F32, name="turned")
+            nc.gpsimd.tensor_tensor(
+                out=kept[:], in0=x[:, :, 0:ROT], in1=rot_cos[:].unsqueeze(1).to_broadcast([P, rows, ROT]), op=MULT
+            )
+            nc.gpsimd.tensor_tensor(
+                out=turned[:, :, 0 : ROT // 2],
+                in0=x[:, :, ROT // 2 : ROT],
+                in1=rot_sin[:, 0 : ROT // 2].unsqueeze(1).to_broadcast([P, rows, ROT // 2]),
+                op=MULT,
+            )
+            nc.gpsimd.tensor_tensor(
+                out=turned[:, :, ROT // 2 : ROT],
+                in0=x[:, :, 0 : ROT // 2],
+                in1=rot_sin[:, ROT // 2 : ROT].unsqueeze(1).to_broadcast([P, rows, ROT // 2]),
+                op=MULT,
+            )
+            nc.gpsimd.tensor_tensor(out=x[:, :, 0:ROT], in0=kept[:], in1=turned[:], op=ADD)
+            nc.sync.dma_start(
+                out=out_3.rearrange("a r e d -> r a (e d)"), in_=k_rot[:].rearrange("r a e d -> r a (e d)")
+            )
+
+        for g in range(GROUPS + 1):
+            if g < GROUPS:
+                regroup_wd(g)
+                transpose_h(g)
+                if g + H_BUFS < GROUPS:
+                    load_wd(g + H_BUFS)
+                    load_h(g + H_BUFS)
+                spread_two_bias_rows(g)
+            if g > 0:
+                quantise_group(g - 1)
+                multiply_c(g - 1)
+        load_chunk(0)
+        nc.sync.dma_start(out=wr_raw[:], in_=W_kr.rearrange("(s p t) n -> p s t n", s=PASSES, p=P, t=PACK))
+        for n in range(1, WU_BUFS):
+            load_chunk(n)
+        regroup_chunk(0)
+        load_chunk(WU_BUFS)
         for a in range(BATCH):
-            for s in range(PASSES):
-                tokens = slice((s * BATCH + a) * P, (s * BATCH + a + 1) * P)
-                nc.tensor.matmul_mx(
-                    out=kr_acc[:, a, :],
-                    lhsT=h_codes[:, tokens].bitcast(FP8X4),
-                    lhsT_scale=h_scales[:, tokens],
-                    rhs=wr_codes[:, s * KR : (s + 1) * KR].bitcast(FP8X4),
-                    rhs_scale=wr_scales[:, s * KR : (s + 1) * KR],
-                    start=(s == 0),
-                    stop=(s == PASSES - 1),
-                )
-        k_rot = keep.tile([P, BATCH, HEADS, D_ROPE], F32, name="k_rot")
-        nc.vector.tensor_tensor(
-            out=k_rot[:].rearrange("r a e d -> r a (e d)"),
-            in0=kr_acc[:],
-            in1=first_bias[:, D_KV:D_HEAD].unsqueeze(1).to_broadcast([P, BATCH, KR]),
-            op=ADD,
-        )
-        x = k_rot[:].rearrange("r a e d -> r (a e) d")
-        rows = BATCH * HEADS
-        kept = keep.tile([P, rows, ROT], F32, name="kept")
-        turned = keep.tile([P, rows, ROT], F32, name="turned")
-        nc.vector.tensor_tensor(
-            out=kept[:], in0=x[:, :, 0:ROT], in1=rot_cos[:].unsqueeze(1).to_broadcast([P, rows, ROT]), op=MULT
-        )
-        nc.vector.tensor_tensor(
-            out=turned[:, :, 0 : ROT // 2],
-            in0=x[:, :, ROT // 2 : ROT],
-            in1=rot_sin[:, 0 : ROT // 2].unsqueeze(1).to_broadcast([P, rows, ROT // 2]),
-            op=MULT,
-        )
-        nc.vector.tensor_tensor(
-            out=turned[:, :, ROT // 2 : ROT],
-            in0=x[:, :, 0 : ROT // 2],
-            in1=rot_sin[:, ROT // 2 : ROT].unsqueeze(1).to_broadcast([P, rows, ROT // 2]),
-            op=MULT,
-        )
-        nc.vector.tensor_tensor(out=x[:, :, 0:ROT], in0=kept[:], in1=turned[:], op=ADD)
-        nc.sync.dma_start(
-            out=out_3.rearrange("a r e d -> r a (e d)"), in_=k_rot[:].rearrange("r a e d -> r a (e d)")
-        )
-
-        for r in range(2 * HEADS):
-            spread_bias_row(r)
-
-        for which, (weight, head_cols, out) in enumerate(((W_uk, D_NOPE, out_0), (W_uv, D_HEAD, out_1))):
-            weight_rows = weight.rearrange("(p t) n -> p t n", t=PACK)
-            for i in range(CHUNKS):
-                wu_raw = wu_in.tile([P, PACK, CHUNK_HEADS * head_cols], BF16, name="wu_raw", tag="wu_raw")
-                nc.sync.dma_start(
-                    out=wu_raw[:],
-                    in_=weight_rows[:, :, i * CHUNK_HEADS * head_cols : (i + 1) * CHUNK_HEADS * head_cols],
-                )
-                wu_grouped = w_stage.tile([P, CHUNK * PACK], BF16, name="wu_grouped", tag="grouped", align_bytes=64)
-                wu_view = wu_grouped[:].rearrange("p (e n t) -> p e n t", e=CHUNK_HEADS, t=PACK)
-                split = head_cols - VECTOR_COLS
-                for e in range(CHUNK_HEADS):
-                    first = e * head_cols
-                    regroup(nc.scalar.copy, wu_view[:, e, 0:split, :], wu_raw[:, :, first : first + split])
-                    regroup(
-                        nc.vector.tensor_copy,
-                        wu_view[:, e, split:head_cols, :],
-                        wu_raw[:, :, first + split : first + head_cols],
-                    )
-                    if head_cols < D_HEAD:
-                        nc.vector.memset(wu_view[:, e, head_cols:D_HEAD, :], 0.0)
-                wu_codes = w_quant.tile([P, CHUNK], U32, name="wu_codes", tag="codes", align_bytes=64)
-                wu_scales = w_quant.tile([P, CHUNK], U8, name="wu_scales", tag="scales", align_bytes=64)
-                quantise(nc, wu_grouped, wu_codes, wu_scales, QUANT_WORDS)
-
-                first_bias_col = (which * HEADS + i * CHUNK_HEADS) * D_HEAD
-                for a in range(BATCH):
-                    result = outs.tile([P, CHUNK_HEADS, D_HEAD], F32, name="result")
-                    result_flat = result[:].rearrange("r e d -> r (e d)")
-                    start = 0
-                    for count in PASS_COLS:
-                        acc = psum.tile([P, count], F32, name="acc", tag="bank")
-                        nc.tensor.matmul_mx(
-                            out=acc[:],
-                            lhsT=c_codes[:, a * P : (a + 1) * P].bitcast(FP8X4),
-                            lhsT_scale=c_scales[:, a * P : (a + 1) * P],
-                            rhs=wu_codes[:, start : start + count].bitcast(FP8X4),
-                            rhs_scale=wu_scales[:, start : start + count],
-                            start=True,
-                            stop=True,
-                        )
-                        nc.vector.tensor_tensor(
-                            out=result_flat[:, start : start + count],
-                            in0=acc[:],
-                            in1=bias_all[:, first_bias_col + start : first_bias_col + start + count],
-                            op=ADD,
-                        )
-                        start += count
-                    if head_cols < D_HEAD:
-                        nc.vector.tensor_copy(
-                            out=result[:, :, head_cols:D_HEAD],
-                            in_=k_rot[:, a, i * CHUNK_HEADS : (i + 1) * CHUNK_HEADS, :],
-                        )
-                    nc.sync.dma_start(
-                        out=out[a, :, i * CHUNK_HEADS : (i + 1) * CHUNK_HEADS, :].rearrange("r e d -> r (e d)"),
-                        in_=result_flat,
-                    )
+            finish_c(a)
+        for a in range(BATCH):
+            transpose_c(a)
+        wr_grouped = regroup_wr()
+        quantise(nc, wr_grouped, wr_codes, wr_scales, QUANT_WORDS)
+        kr_acc = multiply_rope()
+        quantise_chunk(0)
+        quantise(nc, c_grouped, c_codes, c_scales, (BATCH * P,))
+        regroup_chunk(1)
+        load_chunk(WU_BUFS + 1)
+        rotate(kr_acc)
+        for n in range(2 * CHUNKS):
+            spread_two_bias_rows(GROUPS + n)
+            if n + 2 < 2 * CHUNKS:
+                regroup_chunk(n + 2)
+            if n + 2 + WU_BUFS < 2 * CHUNKS:
+                load_chunk(n + 2 + WU_BUFS)
+            multiply_chunk(n)
+            if n + 1 < 2 * CHUNKS:
+                quantise_chunk(n + 1)

@@ -36,7 +36,7 @@ CHUNK = CHUNK_HEADS * D_HEAD
 CHUNKS = HEADS // CHUNK_HEADS
 QUANT_WORDS = (1024, 256)
 PASS_COLS = (512, 512, 256)
-VECTOR_COLS = 128
+GPSIMD_COLS = 192
 WD_SCALAR_COLS = 160
 
 H_BUFS = 3
@@ -267,16 +267,19 @@ def tile_mla_pb_kernel(
         wu_codes = {}
         wu_scales = {}
 
+        def gpsimd_copy(out, in_):
+            nc.gpsimd.tensor_scalar(out=out, in0=in_, scalar1=1.0, scalar2=0.0, op0=MULT, op1=ADD)
+
         def regroup_chunk(n):
             weight, head_cols, out, bias_row, i = chunk_source(n)
             wu_grouped[n] = w_stage.tile([P, CHUNK * PACK], BF16, name="wu_grouped", tag="grouped", align_bytes=64)
             wu_view = wu_grouped[n][:].rearrange("p (e n t) -> p e n t", e=CHUNK_HEADS, t=PACK)
-            split = head_cols - VECTOR_COLS
+            split = head_cols - GPSIMD_COLS
             for e in range(CHUNK_HEADS):
                 first = e * head_cols
                 regroup(nc.scalar.copy, wu_view[:, e, 0:split, :], wu_raw[n][:, :, first : first + split])
                 regroup(
-                    nc.vector.tensor_copy,
+                    gpsimd_copy,
                     wu_view[:, e, split:head_cols, :],
                     wu_raw[n][:, :, first + split : first + head_cols],
                 )
@@ -434,6 +437,6 @@ def tile_mla_pb_kernel(
                 regroup_chunk(n + 2)
             if n + 2 + WU_BUFS < 2 * CHUNKS:
                 load_chunk(n + 2 + WU_BUFS)
-            multiply_chunk(n)
             if n + 1 < 2 * CHUNKS:
                 quantise_chunk(n + 1)
+            multiply_chunk(n)

@@ -72,10 +72,10 @@ def tile_mla_pb_kernel(
     nc = tc.nc
     with ExitStack() as ctx:
         keep = ctx.enter_context(tc.tile_pool(name="keep", bufs=1))
-        h_in = ctx.enter_context(tc.tile_pool(name="h_in", bufs=H_BUFS))
-        wd_in = ctx.enter_context(tc.tile_pool(name="wd_in", bufs=H_BUFS))
+        h_in = ctx.enter_context(tc.tile_pool(name="h_in", bufs=5))
+        wd_in = ctx.enter_context(tc.tile_pool(name="wd_in", bufs=4))
         wu_in = ctx.enter_context(tc.tile_pool(name="wu_in", bufs=WU_BUFS))
-        h_stage = ctx.enter_context(tc.tile_pool(name="h_stage", bufs=2))
+        h_stage = ctx.enter_context(tc.tile_pool(name="h_stage", bufs=3))
         w_stage = ctx.enter_context(tc.tile_pool(name="w_stage", bufs=3))
         w_quant = ctx.enter_context(tc.tile_pool(name="w_quant", bufs=3))
         outs = ctx.enter_context(tc.tile_pool(name="outs", bufs=OUT_BUFS))
@@ -94,12 +94,13 @@ def tile_mla_pb_kernel(
                 in_=h_tokens[:, :, g * GROUP_K : (g + 1) * GROUP_K],
             )
 
-        def load_wd(g):
-            wd_raw[g] = wd_in.tile([P, GROUP, PACK, D_KV], BF16, name="wd_raw")
+        def load_wd(g, first=0, end=GROUP):
+            if first == 0:
+                wd_raw[g] = wd_in.tile([P, GROUP, PACK, D_KV], BF16, name="wd_raw")
             nc.sync.dma_start(
-                out=wd_raw[g][:],
-                in_=W_dkv[g * GROUP_K : (g + 1) * GROUP_K, :].rearrange(
-                    "(c p t) n -> p c t n", c=GROUP, p=P, t=PACK
+                out=wd_raw[g][:, first:end],
+                in_=W_dkv[g * GROUP_K + first * K_PASS : g * GROUP_K + end * K_PASS, :].rearrange(
+                    "(c p t) n -> p c t n", c=end - first, p=P, t=PACK
                 ),
             )
 
@@ -118,8 +119,9 @@ def tile_mla_pb_kernel(
                 ],
             )
 
-        load_wd(0)
+        load_wd(0, 0, 1)
         load_h(0)
+        load_wd(0, 1, GROUP)
         bias_rows = keep.tile([P, D_HEAD], BF16, name="bias_rows")
         nc.vector.memset(bias_rows[:], 0.0)
         nc.sync.dma_start(
@@ -136,9 +138,13 @@ def tile_mla_pb_kernel(
         nc.sync.dma_start(
             out=bias_rows[0:HEADS, 0:D_NOPE], in_=b_uk.rearrange("(r n) -> r n", r=HEADS)
         )
-        for g in range(1, H_BUFS):
-            load_wd(g)
-            load_h(g)
+        load_h(1)
+        load_wd(1)
+        load_h(2)
+        load_wd(2)
+        load_h(3)
+        load_h(4)
+        load_wd(3)
 
         pos_int = keep.tile([P, 1], I32, name="pos_int")
         nc.gpsimd.iota(pos_int[:], pattern=[[0, 1]], base=0, channel_multiplier=1)
@@ -227,26 +233,37 @@ def tile_mla_pb_kernel(
                         )
                 nc.scalar.copy(out=h_grouped_words[:, c], in_=hT[:].rearrange("p a u r -> p a r u"))
 
-        def regroup_wd(g):
-            grouped[g] = w_stage.tile([P, GROUP * D_KV * PACK], BF16, name="wd_grouped", tag="grouped", align_bytes=64)
+        def regroup_wd(g, c):
+            if c == 0:
+                grouped[g] = w_stage.tile([P, GROUP * D_KV * PACK], BF16, name="wd_grouped", tag="grouped", align_bytes=64)
             wd_view = grouped[g][:].rearrange("p (c n t) -> p c n t", c=GROUP, t=PACK)
-            for c in range(GROUP):
-                regroup(nc.scalar.copy, wd_view[:, c, 0:WD_SCALAR_COLS, :], wd_raw[g][:, c, :, 0:WD_SCALAR_COLS])
-                regroup(nc.vector.tensor_copy, wd_view[:, c, WD_SCALAR_COLS:D_KV, :], wd_raw[g][:, c, :, WD_SCALAR_COLS:D_KV])
+            split = WD_SCALAR_COLS
+            regroup(nc.scalar.copy, wd_view[:, c, 0:split, :], wd_raw[g][:, c, :, 0:split])
+            regroup(nc.vector.tensor_copy, wd_view[:, c, split:D_KV, :], wd_raw[g][:, c, :, split:D_KV])
 
-        def quantise_group(g):
+        def quantise_h(g):
             group_words = slice(g * GROUP * BATCH * P, (g + 1) * GROUP * BATCH * P)
             nc.vector.quantize_mx(
                 out=h_codes[:, group_words].bitcast(FP8X4),
                 scales=h_scales[:, group_words],
                 in_=h_grouped[g][:],
             )
-            codes[g] = w_quant.tile([P, GROUP * D_KV], U32, name="wd_codes", tag="codes", align_bytes=64)
-            scales[g] = w_quant.tile([P, GROUP * D_KV], U8, name="wd_scales", tag="scales", align_bytes=64)
-            quantise(nc, grouped[g], codes[g], scales[g], (GROUP * D_KV,))
 
-        def multiply_c(g):
-            for c in range(GROUP):
+        def quantise_wd(g, first, end):
+            if first == 0:
+                codes[g] = w_quant.tile([P, GROUP * D_KV], U32, name="wd_codes", tag="codes", align_bytes=64)
+                scales[g] = w_quant.tile([P, GROUP * D_KV], U8, name="wd_scales", tag="scales", align_bytes=64)
+            words = slice(first * D_KV, end * D_KV)
+            quantise(
+                nc,
+                grouped[g][:, PACK * first * D_KV : PACK * end * D_KV],
+                codes[g][:, words],
+                scales[g][:, words],
+                ((end - first) * D_KV,),
+            )
+
+        def multiply_c(g, first, end):
+            for c in range(first, end):
                 s = g * GROUP + c
                 for a in range(BATCH):
                     tokens = slice((s * BATCH + a) * P, (s * BATCH + a + 1) * P)
@@ -270,19 +287,21 @@ def tile_mla_pb_kernel(
         def gpsimd_copy(out, in_):
             nc.gpsimd.tensor_scalar(out=out, in0=in_, scalar1=1.0, scalar2=0.0, op0=MULT, op1=ADD)
 
-        def regroup_chunk(n):
+        def regroup_chunk(n, vector_cols, gpsimd_cols):
             weight, head_cols, out, bias_row, i = chunk_source(n)
             wu_grouped[n] = w_stage.tile([P, CHUNK * PACK], BF16, name="wu_grouped", tag="grouped", align_bytes=64)
             wu_view = wu_grouped[n][:].rearrange("p (e n t) -> p e n t", e=CHUNK_HEADS, t=PACK)
-            split = head_cols - GPSIMD_COLS
+            ends = (head_cols - gpsimd_cols - vector_cols, head_cols - gpsimd_cols, head_cols)
             for e in range(CHUNK_HEADS):
-                first = e * head_cols
-                regroup(nc.scalar.copy, wu_view[:, e, 0:split, :], wu_raw[n][:, :, first : first + split])
-                regroup(
-                    gpsimd_copy,
-                    wu_view[:, e, split:head_cols, :],
-                    wu_raw[n][:, :, first + split : first + head_cols],
-                )
+                start = 0
+                for copy, end in zip((nc.scalar.copy, nc.vector.tensor_copy, gpsimd_copy), ends):
+                    if start < end:
+                        regroup(
+                            copy,
+                            wu_view[:, e, start:end, :],
+                            wu_raw[n][:, :, e * head_cols + start : e * head_cols + end],
+                        )
+                    start = end
                 if head_cols < D_HEAD:
                     nc.gpsimd.memset(wu_view[:, e, head_cols:D_HEAD, :], 0.0)
 
@@ -294,7 +313,7 @@ def tile_mla_pb_kernel(
         def multiply_chunk(n):
             weight, head_cols, out, bias_row, i = chunk_source(n)
             for a in range(BATCH):
-                result = outs.tile([P, CHUNK_HEADS, D_HEAD], F32, name="result")
+                result = outs.tile([P, CHUNK_HEADS, D_HEAD], F32, name="result", tag="result")
                 result_flat = result[:].rearrange("r e d -> r (e d)")
                 start = 0
                 for count in PASS_COLS:
@@ -326,8 +345,7 @@ def tile_mla_pb_kernel(
                 )
 
         first_bias = bias_all[:, FIRST_ROW * D_HEAD : (FIRST_ROW + 1) * D_HEAD]
-        c_f32 = keep.tile([P, BATCH, D_KV], F32, name="c_f32")
-        c_bf = keep.tile([P, BATCH, PACK, P], BF16, name="c_bf")
+        c_f32 = outs.tile([P, BATCH, D_KV], F32, name="c_f32", tag="result")
         c_grouped = keep.tile([P, BATCH * P * PACK], BF16, name="c_grouped", align_bytes=64)
         c_grouped_view = c_grouped[:].rearrange("q (a r t) -> q a r t", a=BATCH, t=PACK)
 
@@ -336,16 +354,15 @@ def tile_mla_pb_kernel(
             nc.sync.dma_start(out=out_2[a], in_=c_f32[:, a, :])
 
         def transpose_c(a):
-            nc.scalar.copy(out=c_bf[:, a], in_=c_f32[:, a, :].rearrange("r (q t) -> r t q", t=PACK))
-            cT = psum.tile([P, PACK, P], BF16, name="cT", tag="bank")
+            cT = psum.tile([P, PACK, P], F32, name="cT", tag="bank")
             for t in range(PACK):
-                nc.tensor.transpose(cT[:, t, :], c_bf[:, a, t, :], ident_bf[:])
+                nc.tensor.transpose(cT[:, t, :], c_f32[:, a, t:D_KV:PACK], ident_f32[:])
             nc.scalar.copy(out=c_grouped_view[:, a], in_=cT[:].rearrange("q t r -> q r t"))
 
         KR = HEADS * D_ROPE
         wr_raw = keep.tile([P, PASSES, PACK, KR], BF16, name="wr_raw")
-        wr_codes = keep.tile([P, PASSES * KR], U32, name="wr_codes", align_bytes=64)
-        wr_scales = keep.tile([P, PASSES * KR], U8, name="wr_scales", align_bytes=64)
+        wr_codes = w_quant.tile([P, PASSES * KR], U32, name="wr_codes", tag="codes", align_bytes=64)
+        wr_scales = w_quant.tile([P, PASSES * KR], U8, name="wr_scales", tag="scales", align_bytes=64)
 
         def regroup_wr():
             wr_grouped = w_stage.tile([P, PASSES * KR * PACK], BF16, name="wr_grouped", tag="grouped", align_bytes=64)
@@ -402,41 +419,72 @@ def tile_mla_pb_kernel(
                 out=out_3.rearrange("a r e d -> r a (e d)"), in_=k_rot[:].rearrange("r a e d -> r a (e d)")
             )
 
-        for g in range(GROUPS + 1):
-            if g < GROUPS:
-                regroup_wd(g)
-                transpose_h(g)
-                if g + H_BUFS < GROUPS:
-                    load_wd(g + H_BUFS)
-                    load_h(g + H_BUFS)
-                spread_two_bias_rows(g)
-            if g > 0:
-                quantise_group(g - 1)
-                multiply_c(g - 1)
+        regroup_wd(0, 0)
+        transpose_h(0)
+        regroup_wd(0, 1)
+        transpose_h(1)
+        quantise_h(0)
+        quantise_wd(0, 0, GROUP)
+        quantise_h(1)
+        load_wd(4, 0, 1)
+        load_wd(4, 1, GROUP)
+        multiply_c(0, 0, GROUP)
+        regroup_wd(1, 0)
+        regroup_wd(1, 1)
+        transpose_h(2)
+        quantise_wd(1, 0, GROUP)
+        multiply_c(1, 0, GROUP)
+        quantise_h(2)
+        regroup_wd(2, 0)
+        regroup_wd(2, 1)
+        transpose_h(3)
+        quantise_wd(2, 0, GROUP)
+        transpose_h(4)
+        quantise_h(3)
+        regroup_wd(3, 0)
+        regroup_wd(3, 1)
+        multiply_c(2, 0, GROUP)
+        quantise_h(4)
+        quantise_wd(3, 0, GROUP)
+        regroup_wd(4, 0)
+        regroup_wd(4, 1)
+        spread_two_bias_rows(0)
+        multiply_c(3, 0, GROUP)
+        quantise_wd(4, 0, 1)
+        multiply_c(4, 0, 1)
+        quantise_wd(4, 1, GROUP)
+        multiply_c(4, 1, GROUP)
         load_chunk(0)
         nc.sync.dma_start(out=wr_raw[:], in_=W_kr.rearrange("(s p t) n -> p s t n", s=PASSES, p=P, t=PACK))
         for n in range(1, WU_BUFS):
             load_chunk(n)
-        regroup_chunk(0)
+        regroup_chunk(0, 192, 0)
         load_chunk(WU_BUFS)
         for a in range(BATCH):
             finish_c(a)
         for a in range(BATCH):
             transpose_c(a)
-        wr_grouped = regroup_wr()
-        quantise(nc, wr_grouped, wr_codes, wr_scales, QUANT_WORDS)
-        kr_acc = multiply_rope()
         quantise_chunk(0)
         quantise(nc, c_grouped, c_codes, c_scales, (BATCH * P,))
-        regroup_chunk(1)
+        wr_grouped = regroup_wr()
+        spread_two_bias_rows(1)
+        regroup_chunk(1, 0, 192)
         load_chunk(WU_BUFS + 1)
-        rotate(kr_acc)
         for n in range(2 * CHUNKS):
-            spread_two_bias_rows(GROUPS + n)
+            if n == 0:
+                multiply_chunk(n)
+                quantise(nc, wr_grouped, wr_codes, wr_scales, QUANT_WORDS)
+            if n + 2 <= 2 * CHUNKS:
+                spread_two_bias_rows(n + 2)
             if n + 2 < 2 * CHUNKS:
-                regroup_chunk(n + 2)
+                regroup_chunk(n + 2, 0, 192)
             if n + 2 + WU_BUFS < 2 * CHUNKS:
                 load_chunk(n + 2 + WU_BUFS)
             if n + 1 < 2 * CHUNKS:
                 quantise_chunk(n + 1)
-            multiply_chunk(n)
+            if n == 2:
+                kr_acc = multiply_rope()
+            if n > 0:
+                multiply_chunk(n)
+            if n == 2:
+                rotate(kr_acc)

@@ -120,8 +120,8 @@ def tile_mla_pb_kernel(
             )
 
         load_wd(0, 0, 1)
-        load_h(0)
         load_wd(0, 1, GROUP)
+        load_h(0)
         bias_rows = keep.tile([P, D_HEAD], BF16, name="bias_rows")
         nc.vector.memset(bias_rows[:], 0.0)
         nc.sync.dma_start(
@@ -138,13 +138,13 @@ def tile_mla_pb_kernel(
         nc.sync.dma_start(
             out=bias_rows[0:HEADS, 0:D_NOPE], in_=b_uk.rearrange("(r n) -> r n", r=HEADS)
         )
-        load_h(1)
         load_wd(1)
-        load_h(2)
+        load_h(1)
         load_wd(2)
+        load_h(2)
         load_h(3)
-        load_h(4)
         load_wd(3)
+        load_h(4)
 
         pos_int = keep.tile([P, 1], I32, name="pos_int")
         nc.gpsimd.iota(pos_int[:], pattern=[[0, 1]], base=0, channel_multiplier=1)
@@ -420,32 +420,32 @@ def tile_mla_pb_kernel(
             )
 
         regroup_wd(0, 0)
-        transpose_h(0)
         regroup_wd(0, 1)
+        transpose_h(0)
+        quantise_wd(0, 0, GROUP)
+        regroup_wd(1, 0)
+        regroup_wd(1, 1)
         transpose_h(1)
         quantise_h(0)
-        quantise_wd(0, 0, GROUP)
-        quantise_h(1)
+        quantise_wd(1, 0, GROUP)
         load_wd(4, 0, 1)
         load_wd(4, 1, GROUP)
         multiply_c(0, 0, GROUP)
-        regroup_wd(1, 0)
-        regroup_wd(1, 1)
-        transpose_h(2)
-        quantise_wd(1, 0, GROUP)
-        multiply_c(1, 0, GROUP)
-        quantise_h(2)
         regroup_wd(2, 0)
         regroup_wd(2, 1)
-        transpose_h(3)
+        transpose_h(2)
+        quantise_h(1)
         quantise_wd(2, 0, GROUP)
-        transpose_h(4)
-        quantise_h(3)
+        multiply_c(1, 0, GROUP)
+        quantise_h(2)
         regroup_wd(3, 0)
         regroup_wd(3, 1)
+        transpose_h(3)
+        transpose_h(4)
         multiply_c(2, 0, GROUP)
-        quantise_h(4)
+        quantise_h(3)
         quantise_wd(3, 0, GROUP)
+        quantise_h(4)
         regroup_wd(4, 0)
         regroup_wd(4, 1)
         spread_two_bias_rows(0)

@@ -34,14 +34,15 @@ GROUP_K = GROUP * K_PASS
 CHUNK_HEADS = 2
 CHUNK = CHUNK_HEADS * D_HEAD
 CHUNKS = HEADS // CHUNK_HEADS
-QUANT_WORDS = (1024, 256)
 PASS_COLS = (512, 512, 256)
-GPSIMD_COLS = 192
+MAIN_QUANT = (512, 256)
+MAIN_WORDS = sum(MAIN_QUANT)
+LAST_WORDS = CHUNK - MAIN_WORDS
 WD_SCALAR_COLS = 160
 
-H_BUFS = 3
-WU_BUFS = 4
-OUT_BUFS = 6
+RAW_BUFS = 5
+RAW_PASSES = 5
+OUT_BUFS = 5
 BIAS_ROWS = 2 * HEADS + 1
 FIRST_ROW = 2 * HEADS
 
@@ -72,11 +73,10 @@ def tile_mla_pb_kernel(
     nc = tc.nc
     with ExitStack() as ctx:
         keep = ctx.enter_context(tc.tile_pool(name="keep", bufs=1))
-        h_in = ctx.enter_context(tc.tile_pool(name="h_in", bufs=5))
-        wd_in = ctx.enter_context(tc.tile_pool(name="wd_in", bufs=4))
-        wu_in = ctx.enter_context(tc.tile_pool(name="wu_in", bufs=WU_BUFS))
-        h_stage = ctx.enter_context(tc.tile_pool(name="h_stage", bufs=3))
+        raw = ctx.enter_context(tc.tile_pool(name="raw", bufs=RAW_BUFS))
+        h_stage = ctx.enter_context(tc.tile_pool(name="h_stage", bufs=2))
         w_stage = ctx.enter_context(tc.tile_pool(name="w_stage", bufs=3))
+        g_stage = ctx.enter_context(tc.tile_pool(name="g_stage", bufs=1))
         w_quant = ctx.enter_context(tc.tile_pool(name="w_quant", bufs=3))
         outs = ctx.enter_context(tc.tile_pool(name="outs", bufs=OUT_BUFS))
         psum = ctx.enter_context(tc.psum_pool(name="psum", bufs=8))
@@ -86,22 +86,30 @@ def tile_mla_pb_kernel(
         h_raw = {}
         wd_raw = {}
         wu_raw = {}
+        KR = HEADS * D_ROPE
+        wr_raw = keep.tile([P, PASSES, PACK, KR], BF16, name="wr_raw")
+
+        def raw_tile(shape, name):
+            return raw.tile(shape, BF16, name=name, tag="raw", align_bytes=64)
+
+        h_all = []
 
         def load_h(g):
-            h_raw[g] = h_in.tile([P, BATCH * GROUP_K], BF16, name="h_raw")
+            if g == 0:
+                h_all.append(raw_tile([P, GROUPS, BATCH * GROUP_K], "h_all"))
+            h_raw[g] = h_all[0][:, g, :]
             nc.sync.dma_start(
-                out=h_raw[g][:].rearrange("r (a k) -> r a k", a=BATCH),
+                out=h_raw[g].rearrange("r (a k) -> r a k", a=BATCH),
                 in_=h_tokens[:, :, g * GROUP_K : (g + 1) * GROUP_K],
             )
 
-        def load_wd(g, first=0, end=GROUP):
-            if first == 0:
-                wd_raw[g] = wd_in.tile([P, GROUP, PACK, D_KV], BF16, name="wd_raw")
+        def load_wd(first, end):
+            half = first // RAW_PASSES
+            if first % RAW_PASSES == 0:
+                wd_raw[half] = raw_tile([P, RAW_PASSES, PACK, D_KV], "wd_raw")
             nc.sync.dma_start(
-                out=wd_raw[g][:, first:end],
-                in_=W_dkv[g * GROUP_K + first * K_PASS : g * GROUP_K + end * K_PASS, :].rearrange(
-                    "(c p t) n -> p c t n", c=end - first, p=P, t=PACK
-                ),
+                out=wd_raw[half][:, first - half * RAW_PASSES : end - half * RAW_PASSES],
+                in_=W_dkv[first * K_PASS : end * K_PASS, :].rearrange("(c p t) n -> p c t n", c=end - first, p=P, t=PACK),
             )
 
         def chunk_source(n):
@@ -109,18 +117,24 @@ def tile_mla_pb_kernel(
                 return W_uv, D_HEAD, out_1, HEADS + n * CHUNK_HEADS, n
             return W_uk, D_NOPE, out_0, (n - CHUNKS) * CHUNK_HEADS, n - CHUNKS
 
-        def load_chunk(n):
-            weight, head_cols, out, bias_row, i = chunk_source(n)
-            wu_raw[n] = wu_in.tile([P, PACK, CHUNK_HEADS * head_cols], BF16, name="wu_raw")
-            nc.sync.dma_start(
-                out=wu_raw[n][:],
-                in_=weight.rearrange("(p t) n -> p t n", t=PACK)[
-                    :, :, i * CHUNK_HEADS * head_cols : (i + 1) * CHUNK_HEADS * head_cols
-                ],
-            )
+        quads = {}
 
-        load_wd(0, 0, 1)
-        load_wd(0, 1, GROUP)
+        def load_chunks(n, count):
+            weight, head_cols, out, bias_row, i = chunk_source(n)
+            width = CHUNK_HEADS * head_cols
+            if n % 2 == 0:
+                quads[n // 2] = raw_tile([P, 2 * PACK * width], "quad")
+            slab = quads[n // 2][:, n % 2 * PACK * width : (n % 2 + count) * PACK * width]
+            slab = slab.rearrange("p (t n) -> p t n", t=PACK)
+            nc.sync.dma_start(
+                out=slab,
+                in_=weight.rearrange("(p t) n -> p t n", t=PACK)[:, :, i * width : (i + count) * width],
+            )
+            for j in range(count):
+                wu_raw[n + j] = slab[:, :, j * width : (j + 1) * width]
+
+        load_wd(0, 1)
+        load_wd(1, 2)
         load_h(0)
         bias_rows = keep.tile([P, D_HEAD], BF16, name="bias_rows")
         nc.vector.memset(bias_rows[:], 0.0)
@@ -138,13 +152,20 @@ def tile_mla_pb_kernel(
         nc.sync.dma_start(
             out=bias_rows[0:HEADS, 0:D_NOPE], in_=b_uk.rearrange("(r n) -> r n", r=HEADS)
         )
-        load_wd(1)
+        load_wd(2, 4)
         load_h(1)
-        load_wd(2)
+        load_wd(4, 5)
+        load_wd(5, 6)
         load_h(2)
         load_h(3)
-        load_wd(3)
+        load_wd(6, 8)
         load_h(4)
+        load_wd(8, 9)
+        load_wd(9, 10)
+        load_chunks(0, 1)
+        nc.sync.dma_start(out=wr_raw[:], in_=W_kr.rearrange("(s p t) n -> p s t n", s=PASSES, p=P, t=PACK))
+        load_chunks(1, 1)
+        load_chunks(2, 2)
 
         pos_int = keep.tile([P, 1], I32, name="pos_int")
         nc.gpsimd.iota(pos_int[:], pattern=[[0, 1]], base=0, channel_multiplier=1)
@@ -216,7 +237,7 @@ def tile_mla_pb_kernel(
         scales = {}
 
         def transpose_h(g):
-            h_words = h_raw[g][:].bitcast(F32).rearrange("r (a m) -> r a m", a=BATCH)
+            h_words = h_raw[g].bitcast(F32).rearrange("r (a m) -> r a m", a=BATCH)
             h_grouped[g] = h_stage.tile([P, GROUP * BATCH * P * PACK], BF16, name="h_grouped", align_bytes=64)
             h_grouped_words = h_grouped[g][:].bitcast(F32).rearrange(
                 "p (c a r u) -> p c a r u", c=GROUP, a=BATCH, r=P
@@ -233,13 +254,16 @@ def tile_mla_pb_kernel(
                         )
                 nc.scalar.copy(out=h_grouped_words[:, c], in_=hT[:].rearrange("p a u r -> p a r u"))
 
+        def wd_rows(s):
+            return wd_raw[s // RAW_PASSES][:, s % RAW_PASSES]
+
         def regroup_wd(g, c):
             if c == 0:
                 grouped[g] = w_stage.tile([P, GROUP * D_KV * PACK], BF16, name="wd_grouped", tag="grouped", align_bytes=64)
             wd_view = grouped[g][:].rearrange("p (c n t) -> p c n t", c=GROUP, t=PACK)
             split = WD_SCALAR_COLS
-            regroup(nc.scalar.copy, wd_view[:, c, 0:split, :], wd_raw[g][:, c, :, 0:split])
-            regroup(nc.vector.tensor_copy, wd_view[:, c, split:D_KV, :], wd_raw[g][:, c, :, split:D_KV])
+            regroup(nc.scalar.copy, wd_view[:, c, 0:split, :], wd_rows(g * GROUP + c)[:, :, 0:split])
+            regroup(nc.vector.tensor_copy, wd_view[:, c, split:D_KV, :], wd_rows(g * GROUP + c)[:, :, split:D_KV])
 
         def quantise_h(g):
             group_words = slice(g * GROUP * BATCH * P, (g + 1) * GROUP * BATCH * P)
@@ -287,61 +311,78 @@ def tile_mla_pb_kernel(
         def gpsimd_copy(out, in_):
             nc.gpsimd.tensor_scalar(out=out, in0=in_, scalar1=1.0, scalar2=0.0, op0=MULT, op1=ADD)
 
-        def regroup_chunk(n, vector_cols, gpsimd_cols):
-            weight, head_cols, out, bias_row, i = chunk_source(n)
-            wu_grouped[n] = w_stage.tile([P, CHUNK * PACK], BF16, name="wu_grouped", tag="grouped", align_bytes=64)
-            wu_view = wu_grouped[n][:].rearrange("p (e n t) -> p e n t", e=CHUNK_HEADS, t=PACK)
-            ends = (head_cols - gpsimd_cols - vector_cols, head_cols - gpsimd_cols, head_cols)
-            for e in range(CHUNK_HEADS):
-                start = 0
-                for copy, end in zip((nc.scalar.copy, nc.vector.tensor_copy, gpsimd_copy), ends):
-                    if start < end:
-                        regroup(
-                            copy,
-                            wu_view[:, e, start:end, :],
-                            wu_raw[n][:, :, e * head_cols + start : e * head_cols + end],
-                        )
-                    start = end
-                if head_cols < D_HEAD:
-                    nc.gpsimd.memset(wu_view[:, e, head_cols:D_HEAD, :], 0.0)
+        wu_last = {}
+
+        def regroup_main(n):
+            head_cols = chunk_source(n)[1]
+            wu_grouped[n] = w_stage.tile([P, MAIN_WORDS * PACK], BF16, name="wu_grouped", tag="grouped", align_bytes=64)
+            main = wu_grouped[n][:].rearrange("p (n t) -> p n t", t=PACK)
+            split = MAIN_WORDS - D_HEAD + head_cols
+            if head_cols == D_HEAD:
+                regroup(nc.scalar.copy, main[:], wu_raw[n][:, :, 0:split])
+            else:
+                regroup(nc.scalar.copy, main[:, 0:head_cols, :], wu_raw[n][:, :, 0:head_cols])
+                regroup(nc.scalar.copy, main[:, D_HEAD:MAIN_WORDS, :], wu_raw[n][:, :, head_cols:split])
+
+        def regroup_last(n, copy):
+            head_cols = chunk_source(n)[1]
+            wu_last[n] = g_stage.tile([P, LAST_WORDS * PACK], BF16, name="wu_last", align_bytes=64)
+            last = wu_last[n][:].rearrange("p (n t) -> p n t", t=PACK)
+            split = MAIN_WORDS - D_HEAD + head_cols
+            end = CHUNK_HEADS * head_cols
+            regroup(copy, last[:, 0 : end - split, :], wu_raw[n][:, :, split:end])
+            if head_cols < D_HEAD:
+                main = wu_grouped[n][:].rearrange("p (n t) -> p n t", t=PACK)
+                nc.gpsimd.memset(main[:, head_cols:D_HEAD, :], 0.0)
+                nc.gpsimd.memset(last[:, end - split : LAST_WORDS, :], 0.0)
 
         def quantise_chunk(n):
             wu_codes[n] = w_quant.tile([P, CHUNK], U32, name="wu_codes", tag="codes", align_bytes=64)
             wu_scales[n] = w_quant.tile([P, CHUNK], U8, name="wu_scales", tag="scales", align_bytes=64)
-            quantise(nc, wu_grouped[n], wu_codes[n], wu_scales[n], QUANT_WORDS)
+            quantise(nc, wu_grouped[n], wu_codes[n], wu_scales[n], MAIN_QUANT)
+            quantise(nc, wu_last[n], wu_codes[n][:, MAIN_WORDS:CHUNK], wu_scales[n][:, MAIN_WORDS:CHUNK], (LAST_WORDS,))
 
         def multiply_chunk(n):
             weight, head_cols, out, bias_row, i = chunk_source(n)
+            results = []
             for a in range(BATCH):
-                result = outs.tile([P, CHUNK_HEADS, D_HEAD], F32, name="result", tag="result")
-                result_flat = result[:].rearrange("r e d -> r (e d)")
-                start = 0
-                for count in PASS_COLS:
-                    acc = psum.tile([P, count], F32, name="acc", tag="bank")
-                    nc.tensor.matmul_mx(
-                        out=acc[:],
-                        lhsT=c_codes[:, a * P : (a + 1) * P].bitcast(FP8X4),
-                        lhsT_scale=c_scales[:, a * P : (a + 1) * P],
-                        rhs=wu_codes[n][:, start : start + count].bitcast(FP8X4),
-                        rhs_scale=wu_scales[n][:, start : start + count],
-                        start=True,
-                        stop=True,
-                    )
-                    nc.vector.tensor_tensor(
-                        out=result_flat[:, start : start + count],
-                        in0=acc[:],
-                        in1=bias_all[:, bias_row * D_HEAD + start : bias_row * D_HEAD + start + count],
-                        op=ADD,
-                    )
-                    start += count
+                results.append(outs.tile([P, CHUNK_HEADS, D_HEAD], F32, name="result", tag="result"))
+
+            def bank(a, j):
+                start = sum(PASS_COLS[:j])
+                cols = slice(start, start + PASS_COLS[j])
+                acc = psum.tile([P, PASS_COLS[j]], F32, name="acc", tag="bank")
+                nc.tensor.matmul_mx(
+                    out=acc[:],
+                    lhsT=c_codes[:, a * P : (a + 1) * P].bitcast(FP8X4),
+                    lhsT_scale=c_scales[:, a * P : (a + 1) * P],
+                    rhs=wu_codes[n][:, cols].bitcast(FP8X4),
+                    rhs_scale=wu_scales[n][:, cols],
+                    start=True,
+                    stop=True,
+                )
+                part = results[a][:].rearrange("r e d -> r (e d)")[:, cols]
+                bias = bias_all[:, bias_row * D_HEAD + cols.start : bias_row * D_HEAD + cols.stop]
+                return acc, part, bias
+
+            helped = ((1, 0),) if n >= 6 else ()
+            for a, j in helped:
+                acc, part, bias = bank(a, j)
+                nc.scalar.copy(out=part, in_=acc[:])
+                nc.gpsimd.tensor_tensor(out=part, in0=part, in1=bias, op=ADD)
+            for a in range(BATCH):
+                for j in range(len(PASS_COLS)):
+                    if (a, j) not in helped:
+                        acc, part, bias = bank(a, j)
+                        nc.vector.tensor_tensor(out=part, in0=acc[:], in1=bias, op=ADD)
                 if head_cols < D_HEAD:
-                    nc.gpsimd.tensor_copy(
-                        out=result[:, :, head_cols:D_HEAD],
+                    nc.scalar.copy(
+                        out=results[a][:, :, head_cols:D_HEAD],
                         in_=k_rot[:, a, i * CHUNK_HEADS : (i + 1) * CHUNK_HEADS, :],
                     )
                 nc.sync.dma_start(
                     out=out[a, :, i * CHUNK_HEADS : (i + 1) * CHUNK_HEADS, :].rearrange("r e d -> r (e d)"),
-                    in_=result_flat,
+                    in_=results[a][:].rearrange("r e d -> r (e d)"),
                 )
 
         first_bias = bias_all[:, FIRST_ROW * D_HEAD : (FIRST_ROW + 1) * D_HEAD]
@@ -359,18 +400,23 @@ def tile_mla_pb_kernel(
                 nc.tensor.transpose(cT[:, t, :], c_f32[:, a, t:D_KV:PACK], ident_f32[:])
             nc.scalar.copy(out=c_grouped_view[:, a], in_=cT[:].rearrange("q t r -> q r t"))
 
-        KR = HEADS * D_ROPE
-        wr_raw = keep.tile([P, PASSES, PACK, KR], BF16, name="wr_raw")
         wr_codes = w_quant.tile([P, PASSES * KR], U32, name="wr_codes", tag="codes", align_bytes=64)
         wr_scales = w_quant.tile([P, PASSES * KR], U8, name="wr_scales", tag="scales", align_bytes=64)
 
         def regroup_wr():
-            wr_grouped = w_stage.tile([P, PASSES * KR * PACK], BF16, name="wr_grouped", tag="grouped", align_bytes=64)
-            nc.vector.tensor_copy(
-                out=wr_grouped[:].rearrange("p (s c i t) -> p s c t i", s=PASSES, i=4, t=PACK),
-                in_=wr_raw[:].rearrange("p s t (c i) -> p s c t i", i=4),
+            tiles = (
+                w_stage.tile([P, MAIN_WORDS * PACK], BF16, name="wr_grouped", tag="grouped", align_bytes=64),
+                keep.tile([P, LAST_WORDS * PACK], BF16, name="wr_last", align_bytes=64),
             )
-            return wr_grouped
+            first = 0
+            for tile, words in zip(tiles, (MAIN_WORDS, LAST_WORDS)):
+                end = first + words // KR
+                nc.vector.tensor_copy(
+                    out=tile[:].rearrange("p (s c i t) -> p s c t i", s=end - first, i=4, t=PACK),
+                    in_=wr_raw[:, first:end].rearrange("p s t (c i) -> p s c t i", i=4),
+                )
+                first = end
+            return tiles
 
         def multiply_rope():
             kr_acc = psum.tile([P, BATCH, KR], F32, name="kr_acc", tag="bank")
@@ -428,8 +474,6 @@ def tile_mla_pb_kernel(
         transpose_h(1)
         quantise_h(0)
         quantise_wd(1, 0, GROUP)
-        load_wd(4, 0, 1)
-        load_wd(4, 1, GROUP)
         multiply_c(0, 0, GROUP)
         regroup_wd(2, 0)
         regroup_wd(2, 1)
@@ -454,37 +498,37 @@ def tile_mla_pb_kernel(
         multiply_c(4, 0, 1)
         quantise_wd(4, 1, GROUP)
         multiply_c(4, 1, GROUP)
-        load_chunk(0)
-        nc.sync.dma_start(out=wr_raw[:], in_=W_kr.rearrange("(s p t) n -> p s t n", s=PASSES, p=P, t=PACK))
-        for n in range(1, WU_BUFS):
-            load_chunk(n)
-        regroup_chunk(0, 192, 0)
-        load_chunk(WU_BUFS)
+        load_chunks(4, 2)
+        regroup_main(0)
+        regroup_last(0, nc.vector.tensor_copy)
         for a in range(BATCH):
             finish_c(a)
         for a in range(BATCH):
             transpose_c(a)
-        quantise_chunk(0)
-        quantise(nc, c_grouped, c_codes, c_scales, (BATCH * P,))
         wr_grouped = regroup_wr()
+        quantise(nc, c_grouped, c_codes, c_scales, (BATCH * P,))
+        quantise_chunk(0)
         spread_two_bias_rows(1)
-        regroup_chunk(1, 0, 192)
-        load_chunk(WU_BUFS + 1)
+        regroup_main(1)
+        regroup_last(1, gpsimd_copy)
         for n in range(2 * CHUNKS):
             if n == 0:
                 multiply_chunk(n)
-                quantise(nc, wr_grouped, wr_codes, wr_scales, QUANT_WORDS)
+                quantise(nc, wr_grouped[0], wr_codes, wr_scales, MAIN_QUANT)
+                quantise(nc, wr_grouped[1], wr_codes[:, MAIN_WORDS:CHUNK], wr_scales[:, MAIN_WORDS:CHUNK], (LAST_WORDS,))
             if n + 2 <= 2 * CHUNKS:
                 spread_two_bias_rows(n + 2)
             if n + 2 < 2 * CHUNKS:
-                regroup_chunk(n + 2, 0, 192)
-            if n + 2 + WU_BUFS < 2 * CHUNKS:
-                load_chunk(n + 2 + WU_BUFS)
+                regroup_main(n + 2)
             if n + 1 < 2 * CHUNKS:
                 quantise_chunk(n + 1)
+            if n + 2 < 2 * CHUNKS:
+                regroup_last(n + 2, nc.vector.tensor_copy if n == 0 else gpsimd_copy)
             if n == 2:
                 kr_acc = multiply_rope()
             if n > 0:
                 multiply_chunk(n)
+            if n == 1:
+                load_chunks(6, 2)
             if n == 2:
                 rotate(kr_acc)

@@ -38,7 +38,7 @@ PASS_COLS = (512, 512, 256)
 MAIN_QUANT = (512, 256)
 MAIN_WORDS = sum(MAIN_QUANT)
 LAST_WORDS = CHUNK - MAIN_WORDS
-WD_SCALAR_COLS = 160
+WD_SCALAR_COLS = 128
 
 RAW_BUFS = 5
 RAW_PASSES = 5
@@ -165,7 +165,8 @@ def tile_mla_pb_kernel(
         load_chunks(0, 1)
         nc.sync.dma_start(out=wr_raw[:], in_=W_kr.rearrange("(s p t) n -> p s t n", s=PASSES, p=P, t=PACK))
         load_chunks(1, 1)
-        load_chunks(2, 2)
+        load_chunks(2, 1)
+        load_chunks(3, 1)
 
         pos_int = keep.tile([P, 1], I32, name="pos_int")
         nc.gpsimd.iota(pos_int[:], pattern=[[0, 1]], base=0, channel_multiplier=1)

from contextlib import ExitStack

import concourse.mybir as mybir
from concourse.masks import make_identity

F32 = mybir.dt.float32
BF16 = mybir.dt.bfloat16
I32 = mybir.dt.int32
U32 = mybir.dt.uint32
U8 = mybir.dt.uint8
FP8X4 = mybir.dt.float8_e4m3fn_x4
ADD = mybir.AluOpType.add
MULT = mybir.AluOpType.mult
SIN = mybir.ActivationFunctionType.Sin

P = 128
PACK = 4
K_PASS = P * PACK
BATCH = 2
D_MODEL = 5120
D_KV = 512
HEADS = 8
D_HEAD = 640
D_ROPE = 16
D_NOPE = D_HEAD - D_ROPE
ROT = D_ROPE // 2
ROT_SCALE = 40.0

PASSES = D_MODEL // K_PASS
GROUP = 2
GROUPS = PASSES // GROUP
GROUP_K = GROUP * K_PASS

CHUNK_HEADS = 2
CHUNK = CHUNK_HEADS * D_HEAD
CHUNKS = HEADS // CHUNK_HEADS
PASS_COLS = (512, 512, 256)
MAIN_QUANT = (512, 256)
MAIN_WORDS = sum(MAIN_QUANT)
LAST_WORDS = CHUNK - MAIN_WORDS
WD_SCALAR_COLS = 128

RAW_BUFS = 5
RAW_PASSES = 5
OUT_BUFS = 5
BIAS_ROWS = 2 * HEADS + 1
FIRST_ROW = 2 * HEADS

FLOPS = 2 * BATCH * P * (D_MODEL * (D_KV + HEADS * D_ROPE) + D_KV * HEADS * (D_NOPE + D_HEAD))


def regroup(copy, grouped, rows):
    copy(
        out=grouped.rearrange("p (c i) t -> p c t i", i=4),
        in_=rows.rearrange("p t (c i) -> p c t i", i=4),
    )


def quantise(nc, grouped, codes, scales, words):
    start = 0
    for count in words:
        nc.vector.quantize_mx(
            out=codes[:, start : start + count].bitcast(FP8X4),
            scales=scales[:, start : start + count],
            in_=grouped[:, PACK * start : PACK * (start + count)],
        )
        start += count


def tile_mla_pb_kernel(
    tc, h, W_dkv, b_dkv, W_uk, b_uk, W_uv, b_uv, W_kr, b_kr, out_0, out_1, out_2, out_3
):
    nc = tc.nc
    with ExitStack() as ctx:
        keep = ctx.enter_context(tc.tile_pool(name="keep", bufs=1))
        raw = ctx.enter_context(tc.tile_pool(name="raw", bufs=RAW_BUFS))
        h_stage = ctx.enter_context(tc.tile_pool(name="h_stage", bufs=2))
        w_stage = ctx.enter_context(tc.tile_pool(name="w_stage", bufs=3))
        g_stage = ctx.enter_context(tc.tile_pool(name="g_stage", bufs=1))
        w_quant = ctx.enter_context(tc.tile_pool(name="w_quant", bufs=3))
        outs = ctx.enter_context(tc.tile_pool(name="outs", bufs=OUT_BUFS))
        psum = ctx.enter_context(tc.psum_pool(name="psum", bufs=8))
        ctx.enter_context(tc.manual_schedule())

        h_tokens = h.rearrange("a r k -> r a k")
        h_raw = {}
        wd_raw = {}
        wu_raw = {}
        KR = HEADS * D_ROPE
        wr_raw = keep.tile([P, PASSES, PACK, KR], BF16, name="wr_raw")

        def raw_tile(shape, name):
            return raw.tile(shape, BF16, name=name, tag="raw", align_bytes=64)

        h_all = []

        def load_h(g):
            if g == 0:
                h_all.append(raw_tile([P, GROUPS, BATCH * GROUP_K], "h_all"))
            h_raw[g] = h_all[0][:, g, :]
            nc.sync.dma_start(
                out=h_raw[g].rearrange("r (a k) -> r a k", a=BATCH),
                in_=h_tokens[:, :, g * GROUP_K : (g + 1) * GROUP_K],
            )

        def load_wd(first, end):
            half = first // RAW_PASSES
            if first % RAW_PASSES == 0:
                wd_raw[half] = raw_tile([P, RAW_PASSES, PACK, D_KV], "wd_raw")
            nc.sync.dma_start(
                out=wd_raw[half][:, first - half * RAW_PASSES : end - half * RAW_PASSES],
                in_=W_dkv[first * K_PASS : end * K_PASS, :].rearrange("(c p t) n -> p c t n", c=end - first, p=P, t=PACK),
            )

        def chunk_source(n):
            if n < CHUNKS:
                return W_uv, D_HEAD, out_1, HEADS + n * CHUNK_HEADS, n
            return W_uk, D_NOPE, out_0, (n - CHUNKS) * CHUNK_HEADS, n - CHUNKS

        quads = {}

        def load_chunks(n, count):
            weight, head_cols, out, bias_row, i = chunk_source(n)
            width = CHUNK_HEADS * head_cols
            if n % 2 == 0:
                quads[n // 2] = raw_tile([P, 2 * PACK * width], "quad")
            slab = quads[n // 2][:, n % 2 * PACK * width : (n % 2 + count) * PACK * width]
            slab = slab.rearrange("p (t n) -> p t n", t=PACK)
            nc.sync.dma_start(
                out=slab,
                in_=weight.rearrange("(p t) n -> p t n", t=PACK)[:, :, i * width : (i + count) * width],
            )
            for j in range(count):
                wu_raw[n + j] = slab[:, :, j * width : (j + 1) * width]

        load_wd(0, 1)
        load_wd(1, 2)
        load_h(0)
        bias_rows = keep.tile([P, D_HEAD], BF16, name="bias_rows")
        nc.vector.memset(bias_rows[:], 0.0)
        nc.sync.dma_start(
            out=bias_rows[FIRST_ROW : FIRST_ROW + 1, 0:D_KV],
            in_=b_dkv.rearrange("(o n) -> o n", o=1),
        )
        nc.sync.dma_start(
            out=bias_rows[FIRST_ROW : FIRST_ROW + 1, D_KV:D_HEAD],
            in_=b_kr.rearrange("(o n) -> o n", o=1),
        )
        nc.sync.dma_start(
            out=bias_rows[HEADS : 2 * HEADS, :], in_=b_uv.rearrange("(r n) -> r n", r=HEADS)
        )
        nc.sync.dma_start(
            out=bias_rows[0:HEADS, 0:D_NOPE], in_=b_uk.rearrange("(r n) -> r n", r=HEADS)
        )
        load_wd(2, 4)
        load_h(1)
        load_wd(4, 5)
        load_wd(5, 6)
        load_h(2)
        load_h(3)
        load_wd(6, 8)
        load_h(4)
        load_wd(8, 9)
        load_wd(9, 10)
        load_chunks(0, 1)
        nc.sync.dma_start(out=wr_raw[:], in_=W_kr.rearrange("(s p t) n -> p s t n", s=PASSES, p=P, t=PACK))
        load_chunks(1, 1)
        load_chunks(2, 1)
        load_chunks(3, 1)

        pos_int = keep.tile([P, 1], I32, name="pos_int")
        nc.gpsimd.iota(pos_int[:], pattern=[[0, 1]], base=0, channel_multiplier=1)
        ident_f32 = keep.tile([P, P], F32, name="ident_f32")
        make_identity(nc, ident_f32[:])
        ident_bf = keep.tile([P, P], BF16, name="ident_bf")
        make_identity(nc, ident_bf[:])

        bias_all = keep.tile([P, BIAS_ROWS * D_HEAD], BF16, name="bias_all")
        bias_order = [FIRST_ROW] + list(range(HEADS, 2 * HEADS)) + list(range(HEADS))

        def spread_two_bias_rows(step):
            for r in bias_order[2 * step : 2 * step + 2]:
                pick_row = ident_bf[:, r : r + 1].to_broadcast([P, P])
                spread = psum.tile([P, D_HEAD], BF16, name="spread", tag="bank")
                nc.tensor.matmul(
                    out=spread[:, 0:512], lhsT=pick_row, rhs=bias_rows[:, 0:512], start=True, stop=True
                )
                nc.tensor.matmul(
                    out=spread[:, 512:D_HEAD],
                    lhsT=pick_row,
                    rhs=bias_rows[:, 512:D_HEAD],
                    start=True,
                    stop=True,
                )
                nc.scalar.copy(out=bias_all[:, r * D_HEAD : (r + 1) * D_HEAD], in_=spread[:])

        pos = keep.tile([P, 1], F32, name="pos")
        nc.vector.tensor_copy(out=pos[:], in_=pos_int[:])
        half_angle = keep.tile([P, ROT // 2], F32, name="half_angle")
        for j in range(ROT // 2):
            nc.vector.memset(half_angle[:, j : j + 1], 2.0 * ROT_SCALE * 10.0**j)
        nc.vector.reciprocal(out=half_angle[:], in_=half_angle[:])
        nc.vector.tensor_scalar(
            out=half_angle[:], in0=half_angle[:], scalar1=pos[:, 0:1], scalar2=None, op0=MULT
        )
        sin_half = keep.tile([P, ROT // 2], F32, name="sin_half")
        nc.scalar.activation(out=sin_half[:], in_=half_angle[:], func=SIN)
        sin_quarter = keep.tile([P, ROT // 2], F32, name="sin_quarter")
        nc.scalar.activation(out=sin_quarter[:], in_=half_angle[:], func=SIN, scale=0.5)
        rot_cos = keep.tile([P, ROT], F32, name="rot_cos")
        rot_sin = keep.tile([P, ROT], F32, name="rot_sin")

        cos_half = keep.tile([P, ROT // 2], F32, name="cos_half")
        nc.gpsimd.tensor_tensor(out=cos_half[:], in0=sin_quarter[:], in1=sin_quarter[:], op=MULT)
        nc.gpsimd.tensor_scalar(
            out=cos_half[:], in0=cos_half[:], scalar1=-2.0, scalar2=1.0, op0=MULT, op1=ADD
        )
        half_sin = keep.tile([P, ROT // 2], F32, name="half_sin")
        nc.gpsimd.tensor_tensor(out=half_sin[:], in0=sin_half[:], in1=cos_half[:], op=MULT)
        sin_sq = keep.tile([P, ROT // 2], F32, name="sin_sq")
        nc.gpsimd.tensor_tensor(out=sin_sq[:], in0=sin_half[:], in1=sin_half[:], op=MULT)
        for half, sign in ((0, -2.0), (1, 2.0)):
            cols = slice(half * ROT // 2, (half + 1) * ROT // 2)
            nc.gpsimd.tensor_scalar(
                out=rot_cos[:, cols], in0=sin_sq[:], scalar1=-2.0, scalar2=1.0, op0=MULT, op1=ADD
            )
            nc.gpsimd.tensor_scalar(
                out=rot_sin[:, cols], in0=half_sin[:], scalar1=sign, scalar2=None, op0=MULT
            )


        h_codes = keep.tile([P, PASSES * BATCH * P], U32, name="h_codes", align_bytes=64)
        h_scales = keep.tile([P, PASSES * BATCH * P], U8, name="h_scales", align_bytes=64)
        c_acc = [psum.tile([P, D_KV], F32, name="c_acc%d" % a, tag="bank") for a in range(BATCH)]
        h_grouped = {}
        grouped = {}
        codes = {}
        scales = {}

        def transpose_h(g):
            h_words = h_raw[g].bitcast(F32).rearrange("r (a m) -> r a m", a=BATCH)
            h_grouped[g] = h_stage.tile([P, GROUP * BATCH * P * PACK], BF16, name="h_grouped", align_bytes=64)
            h_grouped_words = h_grouped[g][:].bitcast(F32).rearrange(
                "p (c a r u) -> p c a r u", c=GROUP, a=BATCH, r=P
            )
            for c in range(GROUP):
                hT = psum.tile([P, BATCH, 2, P], F32, name="hT", tag="bank")
                first_word = c * K_PASS // 2
                for a in range(BATCH):
                    for u in range(2):
                        nc.tensor.transpose(
                            hT[:, a, u, :],
                            h_words[:, a, first_word + u : first_word + K_PASS // 2 : 2],
                            ident_f32[:],
                        )
                nc.scalar.copy(out=h_grouped_words[:, c], in_=hT[:].rearrange("p a u r -> p a r u"))

        def wd_rows(s):
            return wd_raw[s // RAW_PASSES][:, s % RAW_PASSES]

        def regroup_wd(g, c):
            if c == 0:
                grouped[g] = w_stage.tile([P, GROUP * D_KV * PACK], BF16, name="wd_grouped", tag="grouped", align_bytes=64)
            wd_view = grouped[g][:].rearrange("p (c n t) -> p c n t", c=GROUP, t=PACK)
            split = WD_SCALAR_COLS
            regroup(nc.scalar.copy, wd_view[:, c, 0:split, :], wd_rows(g * GROUP + c)[:, :, 0:split])
            regroup(nc.vector.tensor_copy, wd_view[:, c, split:D_KV, :], wd_rows(g * GROUP + c)[:, :, split:D_KV])

        def quantise_h(g):
            group_words = slice(g * GROUP * BATCH * P, (g + 1) * GROUP * BATCH * P)
            nc.vector.quantize_mx(
                out=h_codes[:, group_words].bitcast(FP8X4),
                scales=h_scales[:, group_words],
                in_=h_grouped[g][:],
            )

        def quantise_wd(g, first, end):
            if first == 0:
                codes[g] = w_quant.tile([P, GROUP * D_KV], U32, name="wd_codes", tag="codes", align_bytes=64)
                scales[g] = w_quant.tile([P, GROUP * D_KV], U8, name="wd_scales", tag="scales", align_bytes=64)
            words = slice(first * D_KV, end * D_KV)
            quantise(
                nc,
                grouped[g][:, PACK * first * D_KV : PACK * end * D_KV],
                codes[g][:, words],
                scales[g][:, words],
                ((end - first) * D_KV,),
            )

        def multiply_c(g, first, end):
            for c in range(first, end):
                s = g * GROUP + c
                for a in range(BATCH):
                    tokens = slice((s * BATCH + a) * P, (s * BATCH + a + 1) * P)
                    nc.tensor.matmul_mx(
                        out=c_acc[a][:],
                        lhsT=h_codes[:, tokens].bitcast(FP8X4),
                        lhsT_scale=h_scales[:, tokens],
                        rhs=codes[g][:, c * D_KV : (c + 1) * D_KV].bitcast(FP8X4),
                        rhs_scale=scales[g][:, c * D_KV : (c + 1) * D_KV],
                        start=(s == 0),
                        stop=(s == PASSES - 1),
                    )

        c_codes = keep.tile([P, BATCH * P], U32, name="c_codes", align_bytes=64)
        c_scales = keep.tile([P, BATCH * P], U8, name="c_scales", align_bytes=64)
        k_rot = keep.tile([P, BATCH, HEADS, D_ROPE], F32, name="k_rot")
        wu_grouped = {}
        wu_codes = {}
        wu_scales = {}

        def gpsimd_copy(out, in_):
            nc.gpsimd.tensor_scalar(out=out, in0=in_, scalar1=1.0, scalar2=0.0, op0=MULT, op1=ADD)

        wu_last = {}

        def regroup_main(n):
            head_cols = chunk_source(n)[1]
            wu_grouped[n] = w_stage.tile([P, MAIN_WORDS * PACK], BF16, name="wu_grouped", tag="grouped", align_bytes=64)
            main = wu_grouped[n][:].rearrange("p (n t) -> p n t", t=PACK)
            split = MAIN_WORDS - D_HEAD + head_cols
            if head_cols == D_HEAD:
                regroup(nc.scalar.copy, main[:], wu_raw[n][:, :, 0:split])
            else:
                regroup(nc.scalar.copy, main[:, 0:head_cols, :], wu_raw[n][:, :, 0:head_cols])
                regroup(nc.scalar.copy, main[:, D_HEAD:MAIN_WORDS, :], wu_raw[n][:, :, head_cols:split])

        def regroup_last(n, copy):
            head_cols = chunk_source(n)[1]
            wu_last[n] = g_stage.tile([P, LAST_WORDS * PACK], BF16, name="wu_last", align_bytes=64)
            last = wu_last[n][:].rearrange("p (n t) -> p n t", t=PACK)
            split = MAIN_WORDS - D_HEAD + head_cols
            end = CHUNK_HEADS * head_cols
            regroup(copy, last[:, 0 : end - split, :], wu_raw[n][:, :, split:end])
            if head_cols < D_HEAD:
                main = wu_grouped[n][:].rearrange("p (n t) -> p n t", t=PACK)
                nc.gpsimd.memset(main[:, head_cols:D_HEAD, :], 0.0)
                nc.gpsimd.memset(last[:, end - split : LAST_WORDS, :], 0.0)

        def quantise_chunk(n):
            wu_codes[n] = w_quant.tile([P, CHUNK], U32, name="wu_codes", tag="codes", align_bytes=64)
            wu_scales[n] = w_quant.tile([P, CHUNK], U8, name="wu_scales", tag="scales", align_bytes=64)
            quantise(nc, wu_grouped[n], wu_codes[n], wu_scales[n], MAIN_QUANT)
            quantise(nc, wu_last[n], wu_codes[n][:, MAIN_WORDS:CHUNK], wu_scales[n][:, MAIN_WORDS:CHUNK], (LAST_WORDS,))

        def multiply_chunk(n):
            weight, head_cols, out, bias_row, i = chunk_source(n)
            results = []
            for a in range(BATCH):
                results.append(outs.tile([P, CHUNK_HEADS, D_HEAD], F32, name="result", tag="result"))

            def bank(a, j):
                start = sum(PASS_COLS[:j])
                cols = slice(start, start + PASS_COLS[j])
                acc = psum.tile([P, PASS_COLS[j]], F32, name="acc", tag="bank")
                nc.tensor.matmul_mx(
                    out=acc[:],
                    lhsT=c_codes[:, a * P : (a + 1) * P].bitcast(FP8X4),
                    lhsT_scale=c_scales[:, a * P : (a + 1) * P],
                    rhs=wu_codes[n][:, cols].bitcast(FP8X4),
                    rhs_scale=wu_scales[n][:, cols],
                    start=True,
                    stop=True,
                )
                part = results[a][:].rearrange("r e d -> r (e d)")[:, cols]
                bias = bias_all[:, bias_row * D_HEAD + cols.start : bias_row * D_HEAD + cols.stop]
                return acc, part, bias

            helped = ((1, 0),) if n >= 6 else ()
            for a, j in helped:
                acc, part, bias = bank(a, j)
                nc.scalar.copy(out=part, in_=acc[:])
                nc.gpsimd.tensor_tensor(out=part, in0=part, in1=bias, op=ADD)
            for a in range(BATCH):
                for j in range(len(PASS_COLS)):
                    if (a, j) not in helped:
                        acc, part, bias = bank(a, j)
                        nc.vector.tensor_tensor(out=part, in0=acc[:], in1=bias, op=ADD)
                if head_cols < D_HEAD:
                    nc.scalar.copy(
                        out=results[a][:, :, head_cols:D_HEAD],
                        in_=k_rot[:, a, i * CHUNK_HEADS : (i + 1) * CHUNK_HEADS, :],
                    )
                nc.sync.dma_start(
                    out=out[a, :, i * CHUNK_HEADS : (i + 1) * CHUNK_HEADS, :].rearrange("r e d -> r (e d)"),
                    in_=results[a][:].rearrange("r e d -> r (e d)"),
                )

        first_bias = bias_all[:, FIRST_ROW * D_HEAD : (FIRST_ROW + 1) * D_HEAD]
        c_f32 = outs.tile([P, BATCH, D_KV], F32, name="c_f32", tag="result")
        c_grouped = keep.tile([P, BATCH * P * PACK], BF16, name="c_grouped", align_bytes=64)
        c_grouped_view = c_grouped[:].rearrange("q (a r t) -> q a r t", a=BATCH, t=PACK)

        def finish_c(a):
            nc.vector.tensor_tensor(out=c_f32[:, a, :], in0=c_acc[a][:], in1=first_bias[:, 0:D_KV], op=ADD)
            nc.sync.dma_start(out=out_2[a], in_=c_f32[:, a, :])

        def transpose_c(a):
            cT = psum.tile([P, PACK, P], F32, name="cT", tag="bank")
            for t in range(PACK):
                nc.tensor.transpose(cT[:, t, :], c_f32[:, a, t:D_KV:PACK], ident_f32[:])
            nc.scalar.copy(out=c_grouped_view[:, a], in_=cT[:].rearrange("q t r -> q r t"))

        wr_codes = w_quant.tile([P, PASSES * KR], U32, name="wr_codes", tag="codes", align_bytes=64)
        wr_scales = w_quant.tile([P, PASSES * KR], U8, name="wr_scales", tag="scales", align_bytes=64)

        def regroup_wr():
            tiles = (
                w_stage.tile([P, MAIN_WORDS * PACK], BF16, name="wr_grouped", tag="grouped", align_bytes=64),
                keep.tile([P, LAST_WORDS * PACK], BF16, name="wr_last", align_bytes=64),
            )
            first = 0
            for tile, words in zip(tiles, (MAIN_WORDS, LAST_WORDS)):
                end = first + words // KR
                nc.vector.tensor_copy(
                    out=tile[:].rearrange("p (s c i t) -> p s c t i", s=end - first, i=4, t=PACK),
                    in_=wr_raw[:, first:end].rearrange("p s t (c i) -> p s c t i", i=4),
                )
                first = end
            return tiles

        def multiply_rope():
            kr_acc = psum.tile([P, BATCH, KR], F32, name="kr_acc", tag="bank")
            for a in range(BATCH):
                for s in range(PASSES):
                    tokens = slice((s * BATCH + a) * P, (s * BATCH + a + 1) * P)
                    nc.tensor.matmul_mx(
                        out=kr_acc[:, a, :],
                        lhsT=h_codes[:, tokens].bitcast(FP8X4),
                        lhsT_scale=h_scales[:, tokens],
                        rhs=wr_codes[:, s * KR : (s + 1) * KR].bitcast(FP8X4),
                        rhs_scale=wr_scales[:, s * KR : (s + 1) * KR],
                        start=(s == 0),
                        stop=(s == PASSES - 1),
                    )
            return kr_acc

        def rotate(kr_acc):
            nc.vector.tensor_tensor(
                out=k_rot[:].rearrange("r a e d -> r a (e d)"),
                in0=kr_acc[:],
                in1=first_bias[:, D_KV:D_HEAD].unsqueeze(1).to_broadcast([P, BATCH, KR]),
                op=ADD,
            )
            x = k_rot[:].rearrange("r a e d -> r (a e) d")
            rows = BATCH * HEADS
            kept = keep.tile([P, rows, ROT], F32, name="kept")
            turned = keep.tile([P, rows, ROT], F32, name="turned")
            nc.gpsimd.tensor_tensor(
                out=kept[:], in0=x[:, :, 0:ROT], in1=rot_cos[:].unsqueeze(1).to_broadcast([P, rows, ROT]), op=MULT
            )
            nc.gpsimd.tensor_tensor(
                out=turned[:, :, 0 : ROT // 2],
                in0=x[:, :, ROT // 2 : ROT],
                in1=rot_sin[:, 0 : ROT // 2].unsqueeze(1).to_broadcast([P, rows, ROT // 2]),
                op=MULT,
            )
            nc.gpsimd.tensor_tensor(
                out=turned[:, :, ROT // 2 : ROT],
                in0=x[:, :, 0 : ROT // 2],
                in1=rot_sin[:, ROT // 2 : ROT].unsqueeze(1).to_broadcast([P, rows, ROT // 2]),
                op=MULT,
            )
            nc.gpsimd.tensor_tensor(out=x[:, :, 0:ROT], in0=kept[:], in1=turned[:], op=ADD)
            nc.sync.dma_start(
                out=out_3.rearrange("a r e d -> r a (e d)"), in_=k_rot[:].rearrange("r a e d -> r a (e d)")
            )

        regroup_wd(0, 0)
        regroup_wd(0, 1)
        transpose_h(0)
        quantise_wd(0, 0, GROUP)
        regroup_wd(1, 0)
        regroup_wd(1, 1)
        transpose_h(1)
        quantise_h(0)
        quantise_wd(1, 0, GROUP)
        multiply_c(0, 0, GROUP)
        regroup_wd(2, 0)
        regroup_wd(2, 1)
        transpose_h(2)
        quantise_h(1)
        quantise_wd(2, 0, GROUP)
        multiply_c(1, 0, GROUP)
        quantise_h(2)
        regroup_wd(3, 0)
        regroup_wd(3, 1)
        transpose_h(3)
        transpose_h(4)
        multiply_c(2, 0, GROUP)
        quantise_h(3)
        quantise_wd(3, 0, GROUP)
        quantise_h(4)
        regroup_wd(4, 0)
        regroup_wd(4, 1)
        spread_two_bias_rows(0)
        multiply_c(3, 0, GROUP)
        quantise_wd(4, 0, 1)
        multiply_c(4, 0, 1)
        quantise_wd(4, 1, GROUP)
        multiply_c(4, 1, GROUP)
        load_chunks(4, 2)
        regroup_main(0)
        regroup_last(0, nc.vector.tensor_copy)
        for a in range(BATCH):
            finish_c(a)
        for a in range(BATCH):
            transpose_c(a)
        wr_grouped = regroup_wr()
        quantise(nc, c_grouped, c_codes, c_scales, (BATCH * P,))
        quantise_chunk(0)
        spread_two_bias_rows(1)
        regroup_main(1)
        regroup_last(1, gpsimd_copy)
        for n in range(2 * CHUNKS):
            if n == 0:
                multiply_chunk(n)
                quantise(nc, wr_grouped[0], wr_codes, wr_scales, MAIN_QUANT)
                quantise(nc, wr_grouped[1], wr_codes[:, MAIN_WORDS:CHUNK], wr_scales[:, MAIN_WORDS:CHUNK], (LAST_WORDS,))
            if n + 2 <= 2 * CHUNKS:
                spread_two_bias_rows(n + 2)
            if n + 2 < 2 * CHUNKS:
                regroup_main(n + 2)
            if n + 1 < 2 * CHUNKS:
                quantise_chunk(n + 1)
            if n + 2 < 2 * CHUNKS:
                regroup_last(n + 2, nc.vector.tensor_copy if n == 0 else gpsimd_copy)
            if n == 2:
                kr_acc = multiply_rope()
            if n > 0:
                multiply_chunk(n)
            if n == 1:
                load_chunks(6, 2)
            if n == 2:
                rotate(kr_acc)
